import numpy as np
import ml_dtypes


def mxq(x, axis, fmt="e4m3"):
    dtype, down = {"e4m3": (ml_dtypes.float8_e4m3fn, 7), "e5m2": (ml_dtypes.float8_e5m2, 14)}[fmt]
    v = np.moveaxis(np.asarray(x, np.float32).astype(ml_dtypes.bfloat16).astype(np.float64), axis, -1)
    blocks = v.reshape(v.shape[:-1] + (-1, 32))
    amax = np.abs(blocks).max(-1, keepdims=True)
    byte = np.maximum(np.where(amax > 0, np.frexp(amax)[1] - 1 + 127, 0) - down, 1)
    scale = np.exp2(byte - 127.0)
    codes = (blocks / scale).astype(np.float32).astype(dtype).astype(np.float64)
    return np.moveaxis((codes * scale).reshape(v.shape), -1, axis)


WIDE = False


def mx_kscale(k):
    if not WIDE:
        return np.ones(k)
    levels = np.array([10, -10, 5, -5, 0])
    a = np.random.permutation(np.resize(levels, k // 512 * 4)).reshape(k // 512, 4)
    idx = np.arange(k)
    return np.exp2(a[idx // 512, idx % 128 // 32])


BF16 = ml_dtypes.bfloat16


def bf(x):
    return np.asarray(x, np.float32).astype(BF16)


def f64(x):
    return np.asarray(x).astype(np.float64)


E2M1 = np.array([0.0, 0.5, 1.0, 1.5, 2.0, 3.0, 4.0, 6.0, -0.0, -0.5, -1.0, -1.5, -2.0, -3.0, -4.0, -6.0])


def pack_weight(w, fmt):
    k, n = w.shape
    w = f64(bf(w)).reshape(k // 32, 32, n)
    amax = np.abs(w).max(1)
    if fmt == "e4m3":
        byte = np.frexp(amax)[1] - 1 + 127 - 7
    else:
        mant, ex = np.frexp(amax / 6.0)
        byte = np.where(mant > 0.5, ex, ex - 1) + 127
    byte = np.clip(np.where(amax > 0, byte, 1), 1, 254)
    scaled = (w * np.exp2(127.0 - byte)[:, None, :]).reshape(k, n).astype(np.float32)
    by_word = np.ascontiguousarray(scaled.reshape(k // 512, 128, 4, n).transpose(0, 1, 3, 2))
    if fmt == "e4m3":
        words = by_word.astype(ml_dtypes.float8_e4m3fn).view(np.uint8)
    else:
        c = by_word.astype(ml_dtypes.float4_e2m1fn).view(np.uint8) & 0xF
        words = c[..., 0::2] | (c[..., 1::2] << 4)
    return np.ascontiguousarray(words), np.ascontiguousarray(byte.astype(np.uint8).reshape(k // 512, 16, n))


def unpack_weight(words, scales, fmt):
    g, p, n, _ = words.shape
    if fmt == "e4m3":
        vals = np.ascontiguousarray(words).view(ml_dtypes.float8_e4m3fn).astype(np.float64)
    else:
        nib = np.empty((g, p, n, 4), np.uint8)
        nib[..., 0::2] = words & 0xF
        nib[..., 1::2] = words >> 4
        vals = E2M1[nib]
    vals = vals * np.repeat(np.exp2(scales.astype(np.float64) - 127.0), 8, axis=1)[..., None]
    return vals.transpose(0, 1, 3, 2).reshape(g * 512, n)

def pack4(w):
    words, scales = pack_weight(w, "e2m1")
    return words.reshape(words.shape[0], 128, -1), scales


def unpack4(words, scales):
    return unpack_weight(words.reshape(words.shape[0], 128, -1, 2), scales, "e2m1")


B, NH, NW, C, K, P = 2, 8, 8, 512, 1024, 4
T = P * P
HAD = np.array([[1.0, 1.0, 1.0, 1.0],
                [1.0, -1.0, 1.0, -1.0],
                [1.0, 1.0, -1.0, -1.0],
                [1.0, -1.0, -1.0, 1.0]])


def setup_inputs():
    s = mx_kscale(C)
    trans = bf(np.random.standard_normal((T, B, NH, NW, C)) * s)
    weight = np.random.standard_normal((T, C, K)) * 0.5 * P / np.sqrt(C) / s[:, None]
    words, scales = pack4(weight.reshape(-1, K))
    bias = bf(np.random.standard_normal((1, 1, 1, K)) * 0.2)
    return {"trans": trans, "weight_words": words, "weight_scales": scales, "bias": bias}


def reference(trans, weight_words, weight_scales, bias):
    x = f64(trans).reshape(T, B * NH * NW, C)
    y = mxq(x, 2, "e4m3") @ unpack4(weight_words, weight_scales).reshape(T, C, K)
    y = y.reshape(P, P, B, NH, NW, K)
    r = np.stack([sum(HAD[p, u] * y[u] for u in range(P)) for p in range(P)])
    z = np.stack([sum(HAD[q, v] * r[:, v] for v in range(P)) for q in range(P)], axis=1) / T
    z = z.transpose(2, 3, 0, 4, 1, 5)
    return z.reshape(B, P * NH, P * NW, K) + f64(bias)

@@ -1,0 +1,178 @@
+from contextlib import ExitStack
+
+import concourse.masks as masks
+import concourse.mybir as mybir
+
+F32 = mybir.dt.float32
+BF16 = mybir.dt.bfloat16
+I32 = mybir.dt.int32
+U32 = mybir.dt.uint32
+U8 = mybir.dt.uint8
+FP8X4 = mybir.dt.float8_e4m3fn_x4
+FP4X4 = mybir.dt.float4_e2m1fn_x4
+
+PARTS = 128
+SIDE = 4
+C_IN = 512
+C_OUT = 1024
+BANK = 512
+HALVES = C_OUT // BANK
+WORDS = C_IN // 2
+PLUS, MINUS = 0, 1
+HADAMARD = ((1, 1, 1, 1), (1, -1, 1, -1), (1, 1, -1, -1), (1, -1, -1, 1))
+
+FLOPS = 2 * SIDE * SIDE * PARTS * C_IN * C_OUT
+
+
+def tile_iwht3layer_pa_e_kernel(tc, trans, weight_words, weight_scales, bias, out):
+    nc = tc.nc
+    mult = mybir.AluOpType.mult
+    add = mybir.AluOpType.add
+    subtract = mybir.AluOpType.subtract
+    copy_fn = mybir.ActivationFunctionType.Copy
+
+    x_dram = trans.rearrange("(u v) b i j c -> v (b i j) u c", v=SIDE)
+    w_dram = weight_words.rearrange("(u v) p n -> v u p n", v=SIDE)
+    s_dram = weight_scales.rearrange("(u v) (quad r) n -> v r quad u n", v=SIDE, r=4)
+    out_dram = out.rearrange("b (i p) (j q) k -> p (b i) j (q k)", p=SIDE, q=SIDE)
+
+    with ExitStack() as ctx:
+        keep = ctx.enter_context(tc.tile_pool(name="keep", bufs=1))
+        stage = ctx.enter_context(tc.tile_pool(name="stage", bufs=2))
+        results = ctx.enter_context(tc.tile_pool(name="results", bufs=3))
+        psum = ctx.enter_context(tc.psum_pool(name="psum", bufs=8))
+
+        def half(h):
+            return slice(h * BANK, (h + 1) * BANK)
+
+        ident = keep.tile([PARTS, PARTS], F32, name="ident")
+        masks.make_identity(nc, ident[:])
+        ones = keep.tile([PARTS, PARTS], BF16, name="ones")
+        nc.vector.memset(ones[:], 1.0)
+        bias_row = keep.tile([PARTS, C_OUT], BF16, name="bias_row")
+        nc.vector.memset(bias_row[:], 0.0)
+        w_planes = keep.tile([PARTS, SIDE * SIDE, C_OUT], U8, name="w_planes", align_bytes=64)
+        nc.vector.memset(w_planes[:].rearrange("p s n -> p (s n)").bitcast(I32), 0)
+
+        nc.scalar.dma_start(out=bias_row[0:1, :], in_=bias.rearrange("a b c k -> (a b c) k"))
+        x_raw = keep.tile([PARTS, SIDE * SIDE, C_IN], BF16, name="x_raw")
+        for v in range(SIDE):
+            nc.sync.dma_start(out=x_raw[:, SIDE * v : SIDE * (v + 1), :], in_=x_dram[v])
+        w_words = keep.tile([PARTS, SIDE * SIDE, 2 * C_OUT], U8, name="w_words", align_bytes=64)
+        for v in range(SIDE):
+            slots = slice(SIDE * v, SIDE * (v + 1))
+            for r in range(4):
+                nc.sync.dma_start(
+                    out=w_planes[r:PARTS:32, slots, :].bitcast(I32), in_=s_dram[v, r].bitcast(I32)
+                )
+            for u in range(SIDE):
+                nc.sync.dma_start(
+                    out=w_words[:, SIDE * v + u, :].bitcast(I32), in_=w_dram[v, u].bitcast(I32)
+                )
+
+        bias_all = keep.tile([PARTS, C_OUT], F32, name="bias_all")
+        for h in range(HALVES):
+            bias_bank = psum.tile([PARTS, BANK], F32, name="bias_bank", tag="bank")
+            nc.tensor.matmul(
+                out=bias_bank[:], lhsT=ones[:], rhs=bias_row[:, half(h)], start=True, stop=True
+            )
+            nc.scalar.copy(out=bias_all[:, half(h)], in_=bias_bank[:])
+
+        x_codes = keep.tile([PARTS, 2, SIDE, SIDE * PARTS], U32, name="x_codes", align_bytes=64)
+        x_planes = keep.tile([PARTS, 2, SIDE, SIDE * PARTS], U8, name="x_planes", align_bytes=64)
+        for v in range(SIDE):
+            x_plus = stage.tile([PARTS, SIDE, PARTS, 2], F32, name="x_plus", align_bytes=64)
+            for pair in range(SIDE // 2):
+                x_bank = psum.tile([PARTS, 2, 2, PARTS], F32, name="x_bank", tag="bank")
+                for s in range(2):
+                    x_words = x_raw[:, SIDE * v + 2 * pair + s, :].bitcast(F32)
+                    for w in range(2):
+                        nc.tensor.transpose(
+                            out=x_bank[:, s, w, :], in_=x_words[:, w:WORDS:2], identity=ident[:]
+                        )
+                copy_out = nc.vector.tensor_copy if pair == 0 else nc.scalar.copy
+                copy_out(
+                    out=x_plus[:, 2 * pair : 2 * pair + 2, :, :],
+                    in_=x_bank[:].rearrange("p s w t -> p s t w"),
+                )
+            x_plus_bf = x_plus[:].rearrange("p u t w -> p (u t w)").bitcast(BF16)
+            x_minus = stage.tile([PARTS, SIDE * C_IN], BF16, name="x_minus", align_bytes=64)
+            nc.scalar.activation(out=x_minus[:], in_=x_plus_bf, func=copy_fn, scale=-1.0)
+            for sign, values in ((PLUS, x_plus_bf), (MINUS, x_minus[:])):
+                nc.vector.quantize_mx(
+                    out=x_codes[:, sign, v, :].bitcast(FP8X4),
+                    scales=x_planes[:, sign, v, :],
+                    in_=values,
+                )
+
+        def mx_pass(acc, p, u, v, h):
+            sign = PLUS if HADAMARD[p][u] > 0 else MINUS
+            tokens = slice(u * PARTS, (u + 1) * PARTS)
+            nc.tensor.matmul_mx(
+                out=acc[:],
+                lhsT=x_codes[:, sign, v, tokens].bitcast(FP8X4),
+                lhsT_scale=x_planes[:, sign, v, tokens],
+                rhs=w_words[:, SIDE * v + u, 2 * h * BANK : 2 * (h + 1) * BANK].bitcast(FP4X4),
+                rhs_scale=w_planes[:, SIDE * v + u, half(h)],
+                start=(u == 0),
+                stop=(u == SIDE - 1),
+            )
+
+        def scaled_sum(dst, acc, factor, other):
+            nc.vector.scalar_tensor_tensor(
+                out=dst, in0=acc[:], scalar=factor, in1=other, op0=mult, op1=add
+            )
+
+        first = keep.tile([PARTS, SIDE, C_OUT], F32, name="first")
+        banks = {}
+        for p in range(SIDE):
+            for h in range(HALVES):
+                banks[(p, h)] = psum.tile([PARTS, BANK], F32, name="acc", tag="bank")
+        for u in range(SIDE):
+            for p in range(SIDE):
+                for h in range(HALVES):
+                    mx_pass(banks[(p, h)], p, u, 0, h)
+        for p in range(SIDE):
+            for h in range(HALVES):
+                scaled_sum(first[:, p, half(h)], banks[(p, h)], 1.0 / 16.0, bias_all[:, half(h)])
+
+        for p in range(SIDE):
+            low = stage.tile([PARTS, 2, C_OUT], F32, name="low")
+            third = stage.tile([PARTS, C_OUT], F32, name="third")
+            high = stage.tile([PARTS, 2, C_OUT], F32, name="high")
+            sums = results.tile([PARTS, 2, C_OUT], F32, name="sums")
+            diffs = results.tile([PARTS, 2, C_OUT], F32, name="diffs")
+            for v in range(1, SIDE):
+                for h in range(HALVES):
+                    acc = psum.tile([PARTS, BANK], F32, name="acc", tag="bank")
+                    for u in range(SIDE):
+                        mx_pass(acc, p, u, v, h)
+                    if v == 1:
+                        scaled_sum(low[:, 0, half(h)], acc, 1.0 / 16.0, first[:, p, half(h)])
+                        scaled_sum(low[:, 1, half(h)], acc, -1.0 / 16.0, first[:, p, half(h)])
+                    elif v == 2:
+                        nc.scalar.activation(
+                            out=third[:, half(h)], in_=acc[:], func=copy_fn, scale=1.0 / 16.0
+                        )
+                    else:
+                        scaled_sum(high[:, 0, half(h)], acc, 1.0 / 16.0, third[:, half(h)])
+                        scaled_sum(high[:, 1, half(h)], acc, -1.0 / 16.0, third[:, half(h)])
+                        nc.vector.tensor_tensor(
+                            out=sums[:, :, half(h)],
+                            in0=low[:, :, half(h)],
+                            in1=high[:, :, half(h)],
+                            op=add,
+                        )
+                        nc.gpsimd.tensor_tensor(
+                            out=diffs[:, :, half(h)],
+                            in0=low[:, :, half(h)],
+                            in1=high[:, :, half(h)],
+                            op=subtract,
+                        )
+            nc.sync.dma_start(
+                out=out_dram[p][:, :, 0 : 2 * C_OUT], in_=sums[:].rearrange("t q k -> t (q k)")
+            )
+            nc.sync.dma_start(
+                out=out_dram[p][:, :, 2 * C_OUT : 4 * C_OUT],
+                in_=diffs[:].rearrange("t q k -> t (q k)"),
+            )

@@ -157,7 +157,7 @@ def tile_iwht3layer_pa_e_kernel(tc, trans, weight_words, weight_scales, bias, ou
                     else:
                         scaled_sum(high[:, 0, half(h)], acc, 1.0 / 16.0, third[:, half(h)])
                         scaled_sum(high[:, 1, half(h)], acc, -1.0 / 16.0, third[:, half(h)])
-                        nc.vector.tensor_tensor(
+                        nc.gpsimd.tensor_tensor(
                             out=sums[:, :, half(h)],
                             in0=low[:, :, half(h)],
                             in1=high[:, :, half(h)],

@@ -157,13 +157,13 @@ def tile_iwht3layer_pa_e_kernel(tc, trans, weight_words, weight_scales, bias, ou
                     else:
                         scaled_sum(high[:, 0, half(h)], acc, 1.0 / 16.0, third[:, half(h)])
                         scaled_sum(high[:, 1, half(h)], acc, -1.0 / 16.0, third[:, half(h)])
-                        nc.gpsimd.tensor_tensor(
+                        nc.vector.tensor_tensor(
                             out=sums[:, :, half(h)],
                             in0=low[:, :, half(h)],
                             in1=high[:, :, half(h)],
                             op=add,
                         )
-                        nc.gpsimd.tensor_tensor(
+                        nc.vector.tensor_tensor(
                             out=diffs[:, :, half(h)],
                             in0=low[:, :, half(h)],
                             in1=high[:, :, half(h)],

@@ -32,66 +32,80 @@ def tile_iwht3layer_pa_e_kernel(tc, trans, weight_words, weight_scales, bias, ou
     copy_fn = mybir.ActivationFunctionType.Copy
 
     x_dram = trans.rearrange("(u v) b i j c -> v (b i j) u c", v=SIDE)
-    w_dram = weight_words.rearrange("(u v) p n -> v u p n", v=SIDE)
+    w_dram = weight_words.rearrange("(u v) p n -> v p u n", v=SIDE)
     s_dram = weight_scales.rearrange("(u v) (quad r) n -> v r quad u n", v=SIDE, r=4)
     out_dram = out.rearrange("b (i p) (j q) k -> p (b i) j (q k)", p=SIDE, q=SIDE)
 
     with ExitStack() as ctx:
         keep = ctx.enter_context(tc.tile_pool(name="keep", bufs=1))
         stage = ctx.enter_context(tc.tile_pool(name="stage", bufs=2))
-        results = ctx.enter_context(tc.tile_pool(name="results", bufs=3))
+        work = ctx.enter_context(tc.tile_pool(name="work", bufs=3))
         psum = ctx.enter_context(tc.psum_pool(name="psum", bufs=8))
 
         def half(h):
             return slice(h * BANK, (h + 1) * BANK)
 
         ident = keep.tile([PARTS, PARTS], F32, name="ident")
-        masks.make_identity(nc, ident[:])
         ones = keep.tile([PARTS, PARTS], BF16, name="ones")
-        nc.vector.memset(ones[:], 1.0)
         bias_row = keep.tile([PARTS, C_OUT], BF16, name="bias_row")
-        nc.vector.memset(bias_row[:], 0.0)
-        w_planes = keep.tile([PARTS, SIDE * SIDE, C_OUT], U8, name="w_planes", align_bytes=64)
-        nc.vector.memset(w_planes[:].rearrange("p s n -> p (s n)").bitcast(I32), 0)
+        bias_all = keep.tile([PARTS, C_OUT], F32, name="bias_all")
+        x_raw = [keep.tile([PARTS, SIDE, C_IN], BF16, name="x_raw%d" % v) for v in range(SIDE)]
+        w_words = [
+            keep.tile([PARTS, SIDE, 2 * C_OUT], U8, name="w_words%d" % v, align_bytes=64)
+            for v in range(SIDE)
+        ]
+        w_planes = [
+            keep.tile([PARTS, SIDE, C_OUT], U8, name="w_planes%d" % v, align_bytes=64)
+            for v in range(SIDE)
+        ]
+        x_codes = [
+            keep.tile([PARTS, 2, SIDE * PARTS], U32, name="x_codes%d" % v, align_bytes=64)
+            for v in range(SIDE)
+        ]
+        x_planes = [
+            keep.tile([PARTS, 2, SIDE * PARTS], U8, name="x_planes%d" % v, align_bytes=64)
+            for v in range(SIDE)
+        ]
 
-        nc.scalar.dma_start(out=bias_row[0:1, :], in_=bias.rearrange("a b c k -> (a b c) k"))
-        x_raw = keep.tile([PARTS, SIDE * SIDE, C_IN], BF16, name="x_raw")
-        for v in range(SIDE):
-            nc.sync.dma_start(out=x_raw[:, SIDE * v : SIDE * (v + 1), :], in_=x_dram[v])
-        w_words = keep.tile([PARTS, SIDE * SIDE, 2 * C_OUT], U8, name="w_words", align_bytes=64)
-        for v in range(SIDE):
-            slots = slice(SIDE * v, SIDE * (v + 1))
+        def zero_planes(v):
+            nc.vector.memset(w_planes[v][:].rearrange("p u n -> p (u n)").bitcast(I32), 0)
+
+        def load_x(v):
+            nc.sync.dma_start(out=x_raw[v][:], in_=x_dram[v])
+
+        def load_w(v):
             for r in range(4):
                 nc.sync.dma_start(
-                    out=w_planes[r:PARTS:32, slots, :].bitcast(I32), in_=s_dram[v, r].bitcast(I32)
+                    out=w_planes[v][r:PARTS:32, :, :].bitcast(I32), in_=s_dram[v, r].bitcast(I32)
                 )
-            for u in range(SIDE):
-                nc.sync.dma_start(
-                    out=w_words[:, SIDE * v + u, :].bitcast(I32), in_=w_dram[v, u].bitcast(I32)
-                )
+            nc.sync.dma_start(out=w_words[v][:].bitcast(I32), in_=w_dram[v].bitcast(I32))
 
-        bias_all = keep.tile([PARTS, C_OUT], F32, name="bias_all")
-        for h in range(HALVES):
-            bias_bank = psum.tile([PARTS, BANK], F32, name="bias_bank", tag="bank")
-            nc.tensor.matmul(
-                out=bias_bank[:], lhsT=ones[:], rhs=bias_row[:, half(h)], start=True, stop=True
-            )
-            nc.scalar.copy(out=bias_all[:, half(h)], in_=bias_bank[:])
+        masks.make_identity(nc, ident[:])
+        with tc.manual_schedule():
+            zero_planes(0)
+            nc.vector.memset(bias_row[:], 0.0)
+            nc.vector.memset(ones[:], 1.0)
+            for v in range(1, SIDE):
+                zero_planes(v)
+            load_x(0)
+            load_w(0)
+            nc.sync.dma_start(out=bias_row[0:1, :], in_=bias.rearrange("a b c k -> (a b c) k"))
+            for v in range(1, SIDE):
+                load_x(v)
+            for v in range(1, SIDE):
+                load_w(v)
 
-        x_codes = keep.tile([PARTS, 2, SIDE, SIDE * PARTS], U32, name="x_codes", align_bytes=64)
-        x_planes = keep.tile([PARTS, 2, SIDE, SIDE * PARTS], U8, name="x_planes", align_bytes=64)
-        for v in range(SIDE):
+        def quantise_x(v):
             x_plus = stage.tile([PARTS, SIDE, PARTS, 2], F32, name="x_plus", align_bytes=64)
             for pair in range(SIDE // 2):
                 x_bank = psum.tile([PARTS, 2, 2, PARTS], F32, name="x_bank", tag="bank")
                 for s in range(2):
-                    x_words = x_raw[:, SIDE * v + 2 * pair + s, :].bitcast(F32)
+                    x_words = x_raw[v][:, 2 * pair + s, :].bitcast(F32)
                     for w in range(2):
                         nc.tensor.transpose(
                             out=x_bank[:, s, w, :], in_=x_words[:, w:WORDS:2], identity=ident[:]
                         )
-                copy_out = nc.vector.tensor_copy if pair == 0 else nc.scalar.copy
-                copy_out(
+                nc.scalar.copy(
                     out=x_plus[:, 2 * pair : 2 * pair + 2, :, :],
                     in_=x_bank[:].rearrange("p s w t -> p s t w"),
                 )
@@ -100,79 +114,77 @@ def tile_iwht3layer_pa_e_kernel(tc, trans, weight_words, weight_scales, bias, ou
             nc.scalar.activation(out=x_minus[:], in_=x_plus_bf, func=copy_fn, scale=-1.0)
             for sign, values in ((PLUS, x_plus_bf), (MINUS, x_minus[:])):
                 nc.vector.quantize_mx(
-                    out=x_codes[:, sign, v, :].bitcast(FP8X4),
-                    scales=x_planes[:, sign, v, :],
+                    out=x_codes[v][:, sign, :].bitcast(FP8X4),
+                    scales=x_planes[v][:, sign, :],
                     in_=values,
                 )
 
-        def mx_pass(acc, p, u, v, h):
-            sign = PLUS if HADAMARD[p][u] > 0 else MINUS
-            tokens = slice(u * PARTS, (u + 1) * PARTS)
-            nc.tensor.matmul_mx(
-                out=acc[:],
-                lhsT=x_codes[:, sign, v, tokens].bitcast(FP8X4),
-                lhsT_scale=x_planes[:, sign, v, tokens],
-                rhs=w_words[:, SIDE * v + u, 2 * h * BANK : 2 * (h + 1) * BANK].bitcast(FP4X4),
-                rhs_scale=w_planes[:, SIDE * v + u, half(h)],
-                start=(u == 0),
-                stop=(u == SIDE - 1),
-            )
+        def mx_group(p, v, h):
+            acc = psum.tile([PARTS, BANK], F32, name="acc", tag="bank")
+            for u in range(SIDE):
+                sign = PLUS if HADAMARD[p][u] > 0 else MINUS
+                tokens = slice(u * PARTS, (u + 1) * PARTS)
+                nc.tensor.matmul_mx(
+                    out=acc[:],
+                    lhsT=x_codes[v][:, sign, tokens].bitcast(FP8X4),
+                    lhsT_scale=x_planes[v][:, sign, tokens],
+                    rhs=w_words[v][:, u, 2 * h * BANK : 2 * (h + 1) * BANK].bitcast(FP4X4),
+                    rhs_scale=w_planes[v][:, u, half(h)],
+                    start=(u == 0),
+                    stop=(u == SIDE - 1),
+                )
+            return acc
 
         def scaled_sum(dst, acc, factor, other):
             nc.vector.scalar_tensor_tensor(
                 out=dst, in0=acc[:], scalar=factor, in1=other, op0=mult, op1=add
             )
 
-        first = keep.tile([PARTS, SIDE, C_OUT], F32, name="first")
-        banks = {}
+        quantise_x(0)
+
+        for h in range(HALVES):
+            bias_bank = psum.tile([PARTS, BANK], F32, name="bias_bank", tag="bank")
+            nc.tensor.matmul(
+                out=bias_bank[:], lhsT=ones[:], rhs=bias_row[:, half(h)], start=True, stop=True
+            )
+            nc.scalar.copy(out=bias_all[:, half(h)], in_=bias_bank[:])
+
+        low = {}
         for p in range(SIDE):
             for h in range(HALVES):
-                banks[(p, h)] = psum.tile([PARTS, BANK], F32, name="acc", tag="bank")
-        for u in range(SIDE):
-            for p in range(SIDE):
-                for h in range(HALVES):
-                    mx_pass(banks[(p, h)], p, u, 0, h)
-        for p in range(SIDE):
-            for h in range(HALVES):
-                scaled_sum(first[:, p, half(h)], banks[(p, h)], 1.0 / 16.0, bias_all[:, half(h)])
+                low[(p, h)] = keep.tile([PARTS, 2, BANK], F32, name="low%d%d" % (p, h))
+                acc = mx_group(p, 0, h)
+                scaled_sum(low[(p, h)][:, 0, :], acc, 1.0 / 16.0, bias_all[:, half(h)])
+            if p + 1 < SIDE:
+                quantise_x(p + 1)
 
         for p in range(SIDE):
-            low = stage.tile([PARTS, 2, C_OUT], F32, name="low")
-            third = stage.tile([PARTS, C_OUT], F32, name="third")
-            high = stage.tile([PARTS, 2, C_OUT], F32, name="high")
-            sums = results.tile([PARTS, 2, C_OUT], F32, name="sums")
-            diffs = results.tile([PARTS, 2, C_OUT], F32, name="diffs")
-            for v in range(1, SIDE):
-                for h in range(HALVES):
-                    acc = psum.tile([PARTS, BANK], F32, name="acc", tag="bank")
-                    for u in range(SIDE):
-                        mx_pass(acc, p, u, v, h)
-                    if v == 1:
-                        scaled_sum(low[:, 0, half(h)], acc, 1.0 / 16.0, first[:, p, half(h)])
-                        scaled_sum(low[:, 1, half(h)], acc, -1.0 / 16.0, first[:, p, half(h)])
-                    elif v == 2:
-                        nc.scalar.activation(
-                            out=third[:, half(h)], in_=acc[:], func=copy_fn, scale=1.0 / 16.0
-                        )
-                    else:
-                        scaled_sum(high[:, 0, half(h)], acc, 1.0 / 16.0, third[:, half(h)])
-                        scaled_sum(high[:, 1, half(h)], acc, -1.0 / 16.0, third[:, half(h)])
-                        nc.vector.tensor_tensor(
-                            out=sums[:, :, half(h)],
-                            in0=low[:, :, half(h)],
-                            in1=high[:, :, half(h)],
-                            op=add,
-                        )
-                        nc.vector.tensor_tensor(
-                            out=diffs[:, :, half(h)],
-                            in0=low[:, :, half(h)],
-                            in1=high[:, :, half(h)],
-                            op=subtract,
-                        )
-            nc.sync.dma_start(
-                out=out_dram[p][:, :, 0 : 2 * C_OUT], in_=sums[:].rearrange("t q k -> t (q k)")
-            )
-            nc.sync.dma_start(
-                out=out_dram[p][:, :, 2 * C_OUT : 4 * C_OUT],
-                in_=diffs[:].rearrange("t q k -> t (q k)"),
-            )
+            for h in range(HALVES):
+                pair_low = low[(p, h)]
+                acc1 = mx_group(p, 1, h)
+                scaled_sum(pair_low[:, 1, :], acc1, -1.0 / 16.0, pair_low[:, 0, :])
+                scaled_sum(pair_low[:, 0, :], acc1, 1.0 / 16.0, pair_low[:, 0, :])
+                acc2 = mx_group(p, 2, h)
+                acc3 = mx_group(p, 3, h)
+                result = work.tile([PARTS, SIDE, BANK], F32, name="result")
+                if (HALVES * p + h) % 3 != 1:
+                    third = work.tile([PARTS, BANK], F32, name="third")
+                    nc.scalar.activation(out=third[:], in_=acc2[:], func=copy_fn, scale=1.0 / 16.0)
+                    high = work.tile([PARTS, 2, BANK], F32, name="high")
+                    scaled_sum(high[:, 0, :], acc3, 1.0 / 16.0, third[:])
+                    scaled_sum(high[:, 1, :], acc3, -1.0 / 16.0, third[:])
+                    nc.gpsimd.tensor_tensor(
+                        out=result[:, 0:2, :], in0=pair_low[:], in1=high[:], op=add
+                    )
+                    nc.gpsimd.tensor_tensor(
+                        out=result[:, 2:4, :], in0=pair_low[:], in1=high[:], op=subtract
+                    )
+                else:
+                    partial = work.tile([PARTS, SIDE, BANK], F32, name="partial")
+                    for q in range(SIDE):
+                        scaled_sum(partial[:, q, :], acc2, HADAMARD[q][2] / 16.0, pair_low[:, q % 2, :])
+                    for q in range(SIDE):
+                        scaled_sum(result[:, q, :], acc3, HADAMARD[q][3] / 16.0, partial[:, q, :])
+                for q in range(SIDE):
+                    columns = slice(q * C_OUT + h * BANK, q * C_OUT + (h + 1) * BANK)
+                    nc.sync.dma_start(out=out_dram[p][:, :, columns], in_=result[:, q, :])

@@ -119,10 +119,11 @@ def tile_iwht3layer_pa_e_kernel(tc, trans, weight_words, weight_scales, bias, ou
                     in_=values,
                 )
 
-        def mx_group(p, v, h):
+        def mx_group(p, q, some_v, h):
             acc = psum.tile([PARTS, BANK], F32, name="acc", tag="bank")
-            for u in range(SIDE):
-                sign = PLUS if HADAMARD[p][u] > 0 else MINUS
+            passes = [(u, v) for v in some_v for u in range(SIDE)]
+            for u, v in passes:
+                sign = PLUS if HADAMARD[p][u] * HADAMARD[q][v] > 0 else MINUS
                 tokens = slice(u * PARTS, (u + 1) * PARTS)
                 nc.tensor.matmul_mx(
                     out=acc[:],
@@ -130,8 +131,8 @@ def tile_iwht3layer_pa_e_kernel(tc, trans, weight_words, weight_scales, bias, ou
                     lhsT_scale=x_planes[v][:, sign, tokens],
                     rhs=w_words[v][:, u, 2 * h * BANK : 2 * (h + 1) * BANK].bitcast(FP4X4),
                     rhs_scale=w_planes[v][:, u, half(h)],
-                    start=(u == 0),
-                    stop=(u == SIDE - 1),
+                    start=((u, v) == passes[0]),
+                    stop=((u, v) == passes[-1]),
                 )
             return acc
 
@@ -153,7 +154,7 @@ def tile_iwht3layer_pa_e_kernel(tc, trans, weight_words, weight_scales, bias, ou
         for p in range(SIDE):
             for h in range(HALVES):
                 low[(p, h)] = keep.tile([PARTS, 2, BANK], F32, name="low%d%d" % (p, h))
-                acc = mx_group(p, 0, h)
+                acc = mx_group(p, 0, (0,), h)
                 scaled_sum(low[(p, h)][:, 0, :], acc, 1.0 / 16.0, bias_all[:, half(h)])
             if p + 1 < SIDE:
                 quantise_x(p + 1)
@@ -161,18 +162,18 @@ def tile_iwht3layer_pa_e_kernel(tc, trans, weight_words, weight_scales, bias, ou
         for p in range(SIDE):
             for h in range(HALVES):
                 pair_low = low[(p, h)]
-                acc1 = mx_group(p, 1, h)
-                scaled_sum(pair_low[:, 1, :], acc1, -1.0 / 16.0, pair_low[:, 0, :])
-                scaled_sum(pair_low[:, 0, :], acc1, 1.0 / 16.0, pair_low[:, 0, :])
-                acc2 = mx_group(p, 2, h)
-                acc3 = mx_group(p, 3, h)
+                acc = mx_group(p, 0, (1,), h)
+                scaled_sum(pair_low[:, 1, :], acc, -1.0 / 16.0, pair_low[:, 0, :])
+                scaled_sum(pair_low[:, 0, :], acc, 1.0 / 16.0, pair_low[:, 0, :])
                 result = work.tile([PARTS, SIDE, BANK], F32, name="result")
                 if (HALVES * p + h) % 3 != 1:
                     third = work.tile([PARTS, BANK], F32, name="third")
-                    nc.scalar.activation(out=third[:], in_=acc2[:], func=copy_fn, scale=1.0 / 16.0)
+                    acc = mx_group(p, 0, (2,), h)
+                    nc.scalar.activation(out=third[:], in_=acc[:], func=copy_fn, scale=1.0 / 16.0)
                     high = work.tile([PARTS, 2, BANK], F32, name="high")
-                    scaled_sum(high[:, 0, :], acc3, 1.0 / 16.0, third[:])
-                    scaled_sum(high[:, 1, :], acc3, -1.0 / 16.0, third[:])
+                    acc = mx_group(p, 0, (3,), h)
+                    scaled_sum(high[:, 0, :], acc, 1.0 / 16.0, third[:])
+                    scaled_sum(high[:, 1, :], acc, -1.0 / 16.0, third[:])
                     nc.gpsimd.tensor_tensor(
                         out=result[:, 0:2, :], in0=pair_low[:], in1=high[:], op=add
                     )
@@ -180,11 +181,10 @@ def tile_iwht3layer_pa_e_kernel(tc, trans, weight_words, weight_scales, bias, ou
                         out=result[:, 2:4, :], in0=pair_low[:], in1=high[:], op=subtract
                     )
                 else:
-                    partial = work.tile([PARTS, SIDE, BANK], F32, name="partial")
-                    for q in range(SIDE):
-                        scaled_sum(partial[:, q, :], acc2, HADAMARD[q][2] / 16.0, pair_low[:, q % 2, :])
-                    for q in range(SIDE):
-                        scaled_sum(result[:, q, :], acc3, HADAMARD[q][3] / 16.0, partial[:, q, :])
+                    for q in range(2):
+                        acc = mx_group(p, q, (2, 3), h)
+                        scaled_sum(result[:, q, :], acc, 1.0 / 16.0, pair_low[:, q, :])
+                        scaled_sum(result[:, q + 2, :], acc, -1.0 / 16.0, pair_low[:, q, :])
                 for q in range(SIDE):
                     columns = slice(q * C_OUT + h * BANK, q * C_OUT + (h + 1) * BANK)
                     nc.sync.dma_start(out=out_dram[p][:, :, columns], in_=result[:, q, :])

@@ -82,14 +82,14 @@ def tile_iwht3layer_pa_e_kernel(tc, trans, weight_words, weight_scales, bias, ou
 
         masks.make_identity(nc, ident[:])
         with tc.manual_schedule():
-            zero_planes(0)
             nc.vector.memset(bias_row[:], 0.0)
+            zero_planes(0)
             nc.vector.memset(ones[:], 1.0)
             for v in range(1, SIDE):
                 zero_planes(v)
             load_x(0)
-            load_w(0)
             nc.sync.dma_start(out=bias_row[0:1, :], in_=bias.rearrange("a b c k -> (a b c) k"))
+            load_w(0)
             for v in range(1, SIDE):
                 load_x(v)
             for v in range(1, SIDE):
@@ -105,7 +105,8 @@ def tile_iwht3layer_pa_e_kernel(tc, trans, weight_words, weight_scales, bias, ou
                         nc.tensor.transpose(
                             out=x_bank[:, s, w, :], in_=x_words[:, w:WORDS:2], identity=ident[:]
                         )
-                nc.scalar.copy(
+                copy_out = nc.vector.tensor_copy if pair == 0 else nc.scalar.copy
+                copy_out(
                     out=x_plus[:, 2 * pair : 2 * pair + 2, :, :],
                     in_=x_bank[:].rearrange("p s w t -> p s t w"),
                 )
@@ -119,11 +120,10 @@ def tile_iwht3layer_pa_e_kernel(tc, trans, weight_words, weight_scales, bias, ou
                     in_=values,
                 )
 
-        def mx_group(p, q, some_v, h):
+        def mx_group(p, v, h):
             acc = psum.tile([PARTS, BANK], F32, name="acc", tag="bank")
-            passes = [(u, v) for v in some_v for u in range(SIDE)]
-            for u, v in passes:
-                sign = PLUS if HADAMARD[p][u] * HADAMARD[q][v] > 0 else MINUS
+            for u in range(SIDE):
+                sign = PLUS if HADAMARD[p][u] > 0 else MINUS
                 tokens = slice(u * PARTS, (u + 1) * PARTS)
                 nc.tensor.matmul_mx(
                     out=acc[:],
@@ -131,8 +131,8 @@ def tile_iwht3layer_pa_e_kernel(tc, trans, weight_words, weight_scales, bias, ou
                     lhsT_scale=x_planes[v][:, sign, tokens],
                     rhs=w_words[v][:, u, 2 * h * BANK : 2 * (h + 1) * BANK].bitcast(FP4X4),
                     rhs_scale=w_planes[v][:, u, half(h)],
-                    start=((u, v) == passes[0]),
-                    stop=((u, v) == passes[-1]),
+                    start=(u == 0),
+                    stop=(u == SIDE - 1),
                 )
             return acc
 
@@ -154,7 +154,7 @@ def tile_iwht3layer_pa_e_kernel(tc, trans, weight_words, weight_scales, bias, ou
         for p in range(SIDE):
             for h in range(HALVES):
                 low[(p, h)] = keep.tile([PARTS, 2, BANK], F32, name="low%d%d" % (p, h))
-                acc = mx_group(p, 0, (0,), h)
+                acc = mx_group(p, 0, h)
                 scaled_sum(low[(p, h)][:, 0, :], acc, 1.0 / 16.0, bias_all[:, half(h)])
             if p + 1 < SIDE:
                 quantise_x(p + 1)
@@ -162,18 +162,18 @@ def tile_iwht3layer_pa_e_kernel(tc, trans, weight_words, weight_scales, bias, ou
         for p in range(SIDE):
             for h in range(HALVES):
                 pair_low = low[(p, h)]
-                acc = mx_group(p, 0, (1,), h)
-                scaled_sum(pair_low[:, 1, :], acc, -1.0 / 16.0, pair_low[:, 0, :])
-                scaled_sum(pair_low[:, 0, :], acc, 1.0 / 16.0, pair_low[:, 0, :])
+                acc1 = mx_group(p, 1, h)
+                scaled_sum(pair_low[:, 1, :], acc1, -1.0 / 16.0, pair_low[:, 0, :])
+                scaled_sum(pair_low[:, 0, :], acc1, 1.0 / 16.0, pair_low[:, 0, :])
+                acc2 = mx_group(p, 2, h)
+                acc3 = mx_group(p, 3, h)
                 result = work.tile([PARTS, SIDE, BANK], F32, name="result")
                 if (HALVES * p + h) % 3 != 1:
                     third = work.tile([PARTS, BANK], F32, name="third")
-                    acc = mx_group(p, 0, (2,), h)
-                    nc.scalar.activation(out=third[:], in_=acc[:], func=copy_fn, scale=1.0 / 16.0)
+                    nc.scalar.activation(out=third[:], in_=acc2[:], func=copy_fn, scale=1.0 / 16.0)
                     high = work.tile([PARTS, 2, BANK], F32, name="high")
-                    acc = mx_group(p, 0, (3,), h)
-                    scaled_sum(high[:, 0, :], acc, 1.0 / 16.0, third[:])
-                    scaled_sum(high[:, 1, :], acc, -1.0 / 16.0, third[:])
+                    scaled_sum(high[:, 0, :], acc3, 1.0 / 16.0, third[:])
+                    scaled_sum(high[:, 1, :], acc3, -1.0 / 16.0, third[:])
                     nc.gpsimd.tensor_tensor(
                         out=result[:, 0:2, :], in0=pair_low[:], in1=high[:], op=add
                     )
@@ -181,10 +181,11 @@ def tile_iwht3layer_pa_e_kernel(tc, trans, weight_words, weight_scales, bias, ou
                         out=result[:, 2:4, :], in0=pair_low[:], in1=high[:], op=subtract
                     )
                 else:
-                    for q in range(2):
-                        acc = mx_group(p, q, (2, 3), h)
-                        scaled_sum(result[:, q, :], acc, 1.0 / 16.0, pair_low[:, q, :])
-                        scaled_sum(result[:, q + 2, :], acc, -1.0 / 16.0, pair_low[:, q, :])
+                    partial = work.tile([PARTS, SIDE, BANK], F32, name="partial")
+                    for q in range(SIDE):
+                        scaled_sum(partial[:, q, :], acc2, HADAMARD[q][2] / 16.0, pair_low[:, q % 2, :])
+                    for q in range(SIDE):
+                        scaled_sum(result[:, q, :], acc3, HADAMARD[q][3] / 16.0, partial[:, q, :])
                 for q in range(SIDE):
                     columns = slice(q * C_OUT + h * BANK, q * C_OUT + (h + 1) * BANK)
                     nc.sync.dma_start(out=out_dram[p][:, :, columns], in_=result[:, q, :])

@@ -159,12 +159,22 @@ def tile_iwht3layer_pa_e_kernel(tc, trans, weight_words, weight_scales, bias, ou
             if p + 1 < SIDE:
                 quantise_x(p + 1)
 
+        def second_coefficient(p, h):
+            pair_low = low[(p, h)]
+            acc1 = mx_group(p, 1, h)
+            scaled_sum(pair_low[:, 1, :], acc1, -1.0 / 16.0, pair_low[:, 0, :])
+            scaled_sum(pair_low[:, 0, :], acc1, 1.0 / 16.0, pair_low[:, 0, :])
+
+        EARLY = 4
+        for p in range(SIDE):
+            for h in range(HALVES):
+                if HALVES * p + h < EARLY:
+                    second_coefficient(p, h)
         for p in range(SIDE):
             for h in range(HALVES):
                 pair_low = low[(p, h)]
-                acc1 = mx_group(p, 1, h)
-                scaled_sum(pair_low[:, 1, :], acc1, -1.0 / 16.0, pair_low[:, 0, :])
-                scaled_sum(pair_low[:, 0, :], acc1, 1.0 / 16.0, pair_low[:, 0, :])
+                if HALVES * p + h >= EARLY:
+                    second_coefficient(p, h)
                 acc2 = mx_group(p, 2, h)
                 acc3 = mx_group(p, 3, h)
                 result = work.tile([PARTS, SIDE, BANK], F32, name="result")

@@ -73,11 +73,13 @@ def tile_iwht3layer_pa_e_kernel(tc, trans, weight_words, weight_scales, bias, ou
         def load_x(v):
             nc.sync.dma_start(out=x_raw[v][:], in_=x_dram[v])
 
-        def load_w(v):
+        def load_scales(v):
             for r in range(4):
                 nc.sync.dma_start(
                     out=w_planes[v][r:PARTS:32, :, :].bitcast(I32), in_=s_dram[v, r].bitcast(I32)
                 )
+
+        def load_words(v):
             nc.sync.dma_start(out=w_words[v][:].bitcast(I32), in_=w_dram[v].bitcast(I32))
 
         masks.make_identity(nc, ident[:])
@@ -89,11 +91,14 @@ def tile_iwht3layer_pa_e_kernel(tc, trans, weight_words, weight_scales, bias, ou
                 zero_planes(v)
             load_x(0)
             nc.sync.dma_start(out=bias_row[0:1, :], in_=bias.rearrange("a b c k -> (a b c) k"))
-            load_w(0)
+            load_scales(0)
+            load_words(0)
             for v in range(1, SIDE):
                 load_x(v)
             for v in range(1, SIDE):
-                load_w(v)
+                load_scales(v)
+            for v in range(1, SIDE):
+                load_words(v)
 
         def quantise_x(v):
             x_plus = stage.tile([PARTS, SIDE, PARTS, 2], F32, name="x_plus", align_bytes=64)

@@ -40,6 +40,7 @@ def tile_iwht3layer_pa_e_kernel(tc, trans, weight_words, weight_scales, bias, ou
         keep = ctx.enter_context(tc.tile_pool(name="keep", bufs=1))
         stage = ctx.enter_context(tc.tile_pool(name="stage", bufs=2))
         work = ctx.enter_context(tc.tile_pool(name="work", bufs=3))
+        lows = ctx.enter_context(tc.tile_pool(name="lows", bufs=6))
         psum = ctx.enter_context(tc.psum_pool(name="psum", bufs=8))
 
         def half(h):
@@ -51,11 +52,17 @@ def tile_iwht3layer_pa_e_kernel(tc, trans, weight_words, weight_scales, bias, ou
         bias_all = keep.tile([PARTS, C_OUT], F32, name="bias_all")
         x_raw = [keep.tile([PARTS, SIDE, C_IN], BF16, name="x_raw%d" % v) for v in range(SIDE)]
         w_words = [
-            keep.tile([PARTS, SIDE, 2 * C_OUT], U8, name="w_words%d" % v, align_bytes=64)
+            [
+                keep.tile([PARTS, SIDE, 2 * BANK], U8, name="w_words%d%d" % (v, h), align_bytes=64)
+                for h in range(HALVES)
+            ]
             for v in range(SIDE)
         ]
         w_planes = [
-            keep.tile([PARTS, SIDE, C_OUT], U8, name="w_planes%d" % v, align_bytes=64)
+            [
+                keep.tile([PARTS, SIDE, BANK], U8, name="w_planes%d%d" % (v, h), align_bytes=64)
+                for h in range(HALVES)
+            ]
             for v in range(SIDE)
         ]
         x_codes = [
@@ -67,38 +74,44 @@ def tile_iwht3layer_pa_e_kernel(tc, trans, weight_words, weight_scales, bias, ou
             for v in range(SIDE)
         ]
 
-        def zero_planes(v):
-            nc.vector.memset(w_planes[v][:].rearrange("p u n -> p (u n)").bitcast(I32), 0)
+        def zero_planes(v, h):
+            nc.vector.memset(w_planes[v][h][:].rearrange("p u n -> p (u n)").bitcast(I32), 0)
 
         def load_x(v):
             nc.sync.dma_start(out=x_raw[v][:], in_=x_dram[v])
 
-        def load_scales(v):
+        def load_scales(v, h):
             for r in range(4):
                 nc.sync.dma_start(
-                    out=w_planes[v][r:PARTS:32, :, :].bitcast(I32), in_=s_dram[v, r].bitcast(I32)
+                    out=w_planes[v][h][r:PARTS:32, :, :].bitcast(I32),
+                    in_=s_dram[v, r][:, :, half(h)].bitcast(I32),
                 )
 
-        def load_words(v):
-            nc.sync.dma_start(out=w_words[v][:].bitcast(I32), in_=w_dram[v].bitcast(I32))
+        def load_words(v, h):
+            nc.sync.dma_start(
+                out=w_words[v][h][:].bitcast(I32),
+                in_=w_dram[v][:, :, 2 * h * BANK : 2 * (h + 1) * BANK].bitcast(I32),
+            )
 
         masks.make_identity(nc, ident[:])
         with tc.manual_schedule():
             nc.vector.memset(bias_row[:], 0.0)
-            zero_planes(0)
+            zero_planes(0, 0)
             nc.vector.memset(ones[:], 1.0)
-            for v in range(1, SIDE):
-                zero_planes(v)
+            for h in range(HALVES):
+                for v in range(SIDE):
+                    if (v, h) != (0, 0):
+                        zero_planes(v, h)
             load_x(0)
             nc.sync.dma_start(out=bias_row[0:1, :], in_=bias.rearrange("a b c k -> (a b c) k"))
-            load_scales(0)
-            load_words(0)
-            for v in range(1, SIDE):
-                load_x(v)
-            for v in range(1, SIDE):
-                load_scales(v)
-            for v in range(1, SIDE):
-                load_words(v)
+            for v in range(SIDE):
+                if v > 0:
+                    load_x(v)
+                load_scales(v, 0)
+                load_words(v, 0)
+            for v in range(SIDE):
+                load_scales(v, 1)
+                load_words(v, 1)
 
         def quantise_x(v):
             x_plus = stage.tile([PARTS, SIDE, PARTS, 2], F32, name="x_plus", align_bytes=64)
@@ -134,8 +147,8 @@ def tile_iwht3layer_pa_e_kernel(tc, trans, weight_words, weight_scales, bias, ou
                     out=acc[:],
                     lhsT=x_codes[v][:, sign, tokens].bitcast(FP8X4),
                     lhsT_scale=x_planes[v][:, sign, tokens],
-                    rhs=w_words[v][:, u, 2 * h * BANK : 2 * (h + 1) * BANK].bitcast(FP4X4),
-                    rhs_scale=w_planes[v][:, u, half(h)],
+                    rhs=w_words[v][h][:, u, :].bitcast(FP4X4),
+                    rhs_scale=w_planes[v][h][:, u, :],
                     start=(u == 0),
                     stop=(u == SIDE - 1),
                 )
@@ -146,61 +159,74 @@ def tile_iwht3layer_pa_e_kernel(tc, trans, weight_words, weight_scales, bias, ou
                 out=dst, in0=acc[:], scalar=factor, in1=other, op0=mult, op1=add
             )
 
-        quantise_x(0)
-
-        for h in range(HALVES):
-            bias_bank = psum.tile([PARTS, BANK], F32, name="bias_bank", tag="bank")
-            nc.tensor.matmul(
-                out=bias_bank[:], lhsT=ones[:], rhs=bias_row[:, half(h)], start=True, stop=True
-            )
-            nc.scalar.copy(out=bias_all[:, half(h)], in_=bias_bank[:])
+        def bias_everywhere():
+            for h in range(HALVES):
+                bias_bank = psum.tile([PARTS, BANK], F32, name="bias_bank", tag="bank")
+                nc.tensor.matmul(
+                    out=bias_bank[:], lhsT=ones[:], rhs=bias_row[:, half(h)], start=True, stop=True
+                )
+                nc.scalar.copy(out=bias_all[:, half(h)], in_=bias_bank[:])
 
         low = {}
-        for p in range(SIDE):
-            for h in range(HALVES):
-                low[(p, h)] = keep.tile([PARTS, 2, BANK], F32, name="low%d%d" % (p, h))
-                acc = mx_group(p, 0, h)
+        kept = {}
+
+        def step(p, v, h):
+            by_vector = (SIDE * h + p) % 3 == 1
+            acc = mx_group(p, v, h)
+            if v == 0:
+                low[(p, h)] = lows.tile([PARTS, 2, BANK], F32, name="low")
                 scaled_sum(low[(p, h)][:, 0, :], acc, 1.0 / 16.0, bias_all[:, half(h)])
-            if p + 1 < SIDE:
-                quantise_x(p + 1)
-
-        def second_coefficient(p, h):
+                return
             pair_low = low[(p, h)]
-            acc1 = mx_group(p, 1, h)
-            scaled_sum(pair_low[:, 1, :], acc1, -1.0 / 16.0, pair_low[:, 0, :])
-            scaled_sum(pair_low[:, 0, :], acc1, 1.0 / 16.0, pair_low[:, 0, :])
-
-        EARLY = 4
-        for p in range(SIDE):
-            for h in range(HALVES):
-                if HALVES * p + h < EARLY:
-                    second_coefficient(p, h)
-        for p in range(SIDE):
-            for h in range(HALVES):
-                pair_low = low[(p, h)]
-                if HALVES * p + h >= EARLY:
-                    second_coefficient(p, h)
-                acc2 = mx_group(p, 2, h)
-                acc3 = mx_group(p, 3, h)
-                result = work.tile([PARTS, SIDE, BANK], F32, name="result")
-                if (HALVES * p + h) % 3 != 1:
-                    third = work.tile([PARTS, BANK], F32, name="third")
-                    nc.scalar.activation(out=third[:], in_=acc2[:], func=copy_fn, scale=1.0 / 16.0)
-                    high = work.tile([PARTS, 2, BANK], F32, name="high")
-                    scaled_sum(high[:, 0, :], acc3, 1.0 / 16.0, third[:])
-                    scaled_sum(high[:, 1, :], acc3, -1.0 / 16.0, third[:])
-                    nc.gpsimd.tensor_tensor(
-                        out=result[:, 0:2, :], in0=pair_low[:], in1=high[:], op=add
-                    )
-                    nc.gpsimd.tensor_tensor(
-                        out=result[:, 2:4, :], in0=pair_low[:], in1=high[:], op=subtract
-                    )
-                else:
+            if v == 1:
+                scaled_sum(pair_low[:, 1, :], acc, -1.0 / 16.0, pair_low[:, 0, :])
+                scaled_sum(pair_low[:, 0, :], acc, 1.0 / 16.0, pair_low[:, 0, :])
+                return
+            if v == 2:
+                if by_vector:
                     partial = work.tile([PARTS, SIDE, BANK], F32, name="partial")
                     for q in range(SIDE):
-                        scaled_sum(partial[:, q, :], acc2, HADAMARD[q][2] / 16.0, pair_low[:, q % 2, :])
-                    for q in range(SIDE):
-                        scaled_sum(result[:, q, :], acc3, HADAMARD[q][3] / 16.0, partial[:, q, :])
+                        scaled_sum(partial[:, q, :], acc, HADAMARD[q][2] / 16.0, pair_low[:, q % 2, :])
+                    kept[(p, h)] = partial
+                else:
+                    third = work.tile([PARTS, BANK], F32, name="third")
+                    nc.scalar.activation(out=third[:], in_=acc[:], func=copy_fn, scale=1.0 / 16.0)
+                    kept[(p, h)] = third
+                return
+            result = work.tile([PARTS, SIDE, BANK], F32, name="result")
+            if by_vector:
+                partial = kept[(p, h)]
                 for q in range(SIDE):
-                    columns = slice(q * C_OUT + h * BANK, q * C_OUT + (h + 1) * BANK)
-                    nc.sync.dma_start(out=out_dram[p][:, :, columns], in_=result[:, q, :])
+                    scaled_sum(result[:, q, :], acc, HADAMARD[q][3] / 16.0, partial[:, q, :])
+            else:
+                third = kept[(p, h)]
+                high = work.tile([PARTS, 2, BANK], F32, name="high")
+                scaled_sum(high[:, 0, :], acc, 1.0 / 16.0, third[:])
+                scaled_sum(high[:, 1, :], acc, -1.0 / 16.0, third[:])
+                nc.gpsimd.tensor_tensor(out=result[:, 0:2, :], in0=pair_low[:], in1=high[:], op=add)
+                nc.gpsimd.tensor_tensor(
+                    out=result[:, 2:4, :], in0=pair_low[:], in1=high[:], op=subtract
+                )
+            for q in range(SIDE):
+                columns = slice(q * C_OUT + h * BANK, q * C_OUT + (h + 1) * BANK)
+                nc.sync.dma_start(out=out_dram[p][:, :, columns], in_=result[:, q, :])
+
+        with tc.manual_schedule(engines={mybir.EngineType.PE}):
+            quantise_x(0)
+            bias_everywhere()
+            step(0, 0, 0)
+            quantise_x(1)
+            for p in range(1, SIDE):
+                step(p, 0, 0)
+            step(0, 1, 0)
+            quantise_x(2)
+            step(1, 1, 0)
+            quantise_x(3)
+            for p in range(2, SIDE):
+                step(p, 1, 0)
+            for p in range(SIDE):
+                for v in range(2, SIDE):
+                    step(p, v, 0)
+            for p in range(SIDE):
+                for v in range(SIDE):
+                    step(p, v, 1)

@@ -33,7 +33,7 @@ def tile_iwht3layer_pa_e_kernel(tc, trans, weight_words, weight_scales, bias, ou
 
     x_dram = trans.rearrange("(u v) b i j c -> v (b i j) u c", v=SIDE)
     w_dram = weight_words.rearrange("(u v) p n -> v p u n", v=SIDE)
-    s_dram = weight_scales.rearrange("(u v) (quad r) n -> v r quad u n", v=SIDE, r=4)
+    s_dram = weight_scales.rearrange("t (quad r) n -> r quad t n", r=4)
     out_dram = out.rearrange("b (i p) (j q) k -> p (b i) j (q k)", p=SIDE, q=SIDE)
 
     with ExitStack() as ctx:
@@ -59,11 +59,8 @@ def tile_iwht3layer_pa_e_kernel(tc, trans, weight_words, weight_scales, bias, ou
             for v in range(SIDE)
         ]
         w_planes = [
-            [
-                keep.tile([PARTS, SIDE, BANK], U8, name="w_planes%d%d" % (v, h), align_bytes=64)
-                for h in range(HALVES)
-            ]
-            for v in range(SIDE)
+            keep.tile([PARTS, SIDE * SIDE, BANK], U8, name="w_planes%d" % h, align_bytes=64)
+            for h in range(HALVES)
         ]
         x_codes = [
             keep.tile([PARTS, 2, SIDE * PARTS], U32, name="x_codes%d" % v, align_bytes=64)
@@ -74,17 +71,17 @@ def tile_iwht3layer_pa_e_kernel(tc, trans, weight_words, weight_scales, bias, ou
             for v in range(SIDE)
         ]
 
-        def zero_planes(v, h):
-            nc.vector.memset(w_planes[v][h][:].rearrange("p u n -> p (u n)").bitcast(I32), 0)
+        def zero_planes(h):
+            nc.vector.memset(w_planes[h][:].rearrange("p t n -> p (t n)").bitcast(I32), 0)
 
         def load_x(v):
             nc.sync.dma_start(out=x_raw[v][:], in_=x_dram[v])
 
-        def load_scales(v, h):
+        def load_scales(h):
             for r in range(4):
                 nc.sync.dma_start(
-                    out=w_planes[v][h][r:PARTS:32, :, :].bitcast(I32),
-                    in_=s_dram[v, r][:, :, half(h)].bitcast(I32),
+                    out=w_planes[h][r:PARTS:32, :, :].bitcast(I32),
+                    in_=s_dram[r][:, :, half(h)].bitcast(I32),
                 )
 
         def load_words(v, h):
@@ -95,22 +92,22 @@ def tile_iwht3layer_pa_e_kernel(tc, trans, weight_words, weight_scales, bias, ou
 
         masks.make_identity(nc, ident[:])
         with tc.manual_schedule():
+            zero_planes(0)
             nc.vector.memset(bias_row[:], 0.0)
-            zero_planes(0, 0)
             nc.vector.memset(ones[:], 1.0)
-            for h in range(HALVES):
-                for v in range(SIDE):
-                    if (v, h) != (0, 0):
-                        zero_planes(v, h)
+            zero_planes(1)
             load_x(0)
+            load_x(1)
+            load_scales(0)
             nc.sync.dma_start(out=bias_row[0:1, :], in_=bias.rearrange("a b c k -> (a b c) k"))
+            load_words(0, 0)
+            load_x(2)
+            load_words(1, 0)
+            load_x(3)
+            load_words(2, 0)
+            load_words(3, 0)
+            load_scales(1)
             for v in range(SIDE):
-                if v > 0:
-                    load_x(v)
-                load_scales(v, 0)
-                load_words(v, 0)
-            for v in range(SIDE):
-                load_scales(v, 1)
                 load_words(v, 1)
 
         def quantise_x(v):
@@ -123,15 +120,16 @@ def tile_iwht3layer_pa_e_kernel(tc, trans, weight_words, weight_scales, bias, ou
                         nc.tensor.transpose(
                             out=x_bank[:, s, w, :], in_=x_words[:, w:WORDS:2], identity=ident[:]
                         )
-                copy_out = nc.vector.tensor_copy if pair == 0 else nc.scalar.copy
+                copy_out = nc.vector.tensor_copy if (pair == 0 and v == 0) else nc.scalar.copy
                 copy_out(
                     out=x_plus[:, 2 * pair : 2 * pair + 2, :, :],
                     in_=x_bank[:].rearrange("p s w t -> p s t w"),
                 )
             x_plus_bf = x_plus[:].rearrange("p u t w -> p (u t w)").bitcast(BF16)
             x_minus = stage.tile([PARTS, SIDE * C_IN], BF16, name="x_minus", align_bytes=64)
-            nc.scalar.activation(out=x_minus[:], in_=x_plus_bf, func=copy_fn, scale=-1.0)
             for sign, values in ((PLUS, x_plus_bf), (MINUS, x_minus[:])):
+                if sign == MINUS:
+                    nc.vector.tensor_scalar_mul(out=x_minus[:], in0=x_plus_bf, scalar1=-1.0)
                 nc.vector.quantize_mx(
                     out=x_codes[v][:, sign, :].bitcast(FP8X4),
                     scales=x_planes[v][:, sign, :],
@@ -148,7 +146,7 @@ def tile_iwht3layer_pa_e_kernel(tc, trans, weight_words, weight_scales, bias, ou
                     lhsT=x_codes[v][:, sign, tokens].bitcast(FP8X4),
                     lhsT_scale=x_planes[v][:, sign, tokens],
                     rhs=w_words[v][h][:, u, :].bitcast(FP4X4),
-                    rhs_scale=w_planes[v][h][:, u, :],
+                    rhs_scale=w_planes[h][:, SIDE * u + v, :],
                     start=(u == 0),
                     stop=(u == SIDE - 1),
                 )
@@ -171,7 +169,9 @@ def tile_iwht3layer_pa_e_kernel(tc, trans, weight_words, weight_scales, bias, ou
         kept = {}
 
         def step(p, v, h):
-            by_vector = (SIDE * h + p) % 3 == 1
+            number = SIDE * h + p
+            by_gpsimd = 0 if number == SIDE * HALVES - 1 else (4 if number % 2 == 0 else 2)
+            chain = [q for q in range(SIDE) if by_gpsimd == 0 or (by_gpsimd == 2 and q % 2 == 1)]
             acc = mx_group(p, v, h)
             if v == 0:
                 low[(p, h)] = lows.tile([PARTS, 2, BANK], F32, name="low")
@@ -183,49 +183,54 @@ def tile_iwht3layer_pa_e_kernel(tc, trans, weight_words, weight_scales, bias, ou
                 scaled_sum(pair_low[:, 0, :], acc, 1.0 / 16.0, pair_low[:, 0, :])
                 return
             if v == 2:
-                if by_vector:
-                    partial = work.tile([PARTS, SIDE, BANK], F32, name="partial")
-                    for q in range(SIDE):
-                        scaled_sum(partial[:, q, :], acc, HADAMARD[q][2] / 16.0, pair_low[:, q % 2, :])
-                    kept[(p, h)] = partial
-                else:
+                if by_gpsimd > 0:
                     third = work.tile([PARTS, BANK], F32, name="third")
                     nc.scalar.activation(out=third[:], in_=acc[:], func=copy_fn, scale=1.0 / 16.0)
-                    kept[(p, h)] = third
+                    kept[(p, h, "third")] = third
+                if chain:
+                    partial = work.tile([PARTS, SIDE, BANK], F32, name="partial")
+                    for q in chain:
+                        scaled_sum(partial[:, q, :], acc, HADAMARD[q][2] / 16.0, pair_low[:, q % 2, :])
+                    kept[(p, h, "partial")] = partial
                 return
             result = work.tile([PARTS, SIDE, BANK], F32, name="result")
-            if by_vector:
-                partial = kept[(p, h)]
-                for q in range(SIDE):
-                    scaled_sum(result[:, q, :], acc, HADAMARD[q][3] / 16.0, partial[:, q, :])
-            else:
-                third = kept[(p, h)]
+            if by_gpsimd > 0:
+                third = kept[(p, h, "third")]
                 high = work.tile([PARTS, 2, BANK], F32, name="high")
                 scaled_sum(high[:, 0, :], acc, 1.0 / 16.0, third[:])
-                scaled_sum(high[:, 1, :], acc, -1.0 / 16.0, third[:])
-                nc.gpsimd.tensor_tensor(out=result[:, 0:2, :], in0=pair_low[:], in1=high[:], op=add)
-                nc.gpsimd.tensor_tensor(
-                    out=result[:, 2:4, :], in0=pair_low[:], in1=high[:], op=subtract
-                )
+                if by_gpsimd == 4:
+                    scaled_sum(high[:, 1, :], acc, -1.0 / 16.0, third[:])
+                    nc.gpsimd.tensor_tensor(
+                        out=result[:, 0:2, :], in0=pair_low[:], in1=high[:], op=add
+                    )
+                    nc.gpsimd.tensor_tensor(
+                        out=result[:, 2:4, :], in0=pair_low[:], in1=high[:], op=subtract
+                    )
+                else:
+                    nc.gpsimd.tensor_tensor(
+                        out=result[:, 0, :], in0=pair_low[:, 0, :], in1=high[:, 0, :], op=add
+                    )
+                    nc.gpsimd.tensor_tensor(
+                        out=result[:, 2, :], in0=pair_low[:, 0, :], in1=high[:, 0, :], op=subtract
+                    )
+            for q in chain:
+                scaled_sum(result[:, q, :], acc, HADAMARD[q][3] / 16.0, kept[(p, h, "partial")][:, q, :])
             for q in range(SIDE):
                 columns = slice(q * C_OUT + h * BANK, q * C_OUT + (h + 1) * BANK)
                 nc.sync.dma_start(out=out_dram[p][:, :, columns], in_=result[:, q, :])
 
+        FIRST = 2
         with tc.manual_schedule(engines={mybir.EngineType.PE}):
             quantise_x(0)
-            bias_everywhere()
-            step(0, 0, 0)
             quantise_x(1)
-            for p in range(1, SIDE):
-                step(p, 0, 0)
-            step(0, 1, 0)
-            quantise_x(2)
-            step(1, 1, 0)
-            quantise_x(3)
-            for p in range(2, SIDE):
-                step(p, 1, 0)
-            for p in range(SIDE):
-                for v in range(2, SIDE):
+            bias_everywhere()
+            for v in range(SIDE):
+                for p in range(FIRST):
+                    step(p, v, 0)
+                if v + 2 < SIDE:
+                    quantise_x(v + 2)
+            for p in range(FIRST, SIDE):
+                for v in range(SIDE):
                     step(p, v, 0)
             for p in range(SIDE):
                 for v in range(SIDE):

@@ -33,7 +33,7 @@ def tile_iwht3layer_pa_e_kernel(tc, trans, weight_words, weight_scales, bias, ou
 
     x_dram = trans.rearrange("(u v) b i j c -> v (b i j) u c", v=SIDE)
     w_dram = weight_words.rearrange("(u v) p n -> v p u n", v=SIDE)
-    s_dram = weight_scales.rearrange("t (quad r) n -> r quad t n", r=4)
+    s_dram = weight_scales.rearrange("(u v) (quad r) n -> v r quad u n", v=SIDE, r=4)
     out_dram = out.rearrange("b (i p) (j q) k -> p (b i) j (q k)", p=SIDE, q=SIDE)
 
     with ExitStack() as ctx:
@@ -59,8 +59,11 @@ def tile_iwht3layer_pa_e_kernel(tc, trans, weight_words, weight_scales, bias, ou
             for v in range(SIDE)
         ]
         w_planes = [
-            keep.tile([PARTS, SIDE * SIDE, BANK], U8, name="w_planes%d" % h, align_bytes=64)
-            for h in range(HALVES)
+            [
+                keep.tile([PARTS, SIDE, BANK], U8, name="w_planes%d%d" % (v, h), align_bytes=64)
+                for h in range(HALVES)
+            ]
+            for v in range(SIDE)
         ]
         x_codes = [
             keep.tile([PARTS, 2, SIDE * PARTS], U32, name="x_codes%d" % v, align_bytes=64)
@@ -71,17 +74,17 @@ def tile_iwht3layer_pa_e_kernel(tc, trans, weight_words, weight_scales, bias, ou
             for v in range(SIDE)
         ]
 
-        def zero_planes(h):
-            nc.vector.memset(w_planes[h][:].rearrange("p t n -> p (t n)").bitcast(I32), 0)
+        def zero_planes(v, h):
+            nc.vector.memset(w_planes[v][h][:].rearrange("p u n -> p (u n)").bitcast(I32), 0)
 
         def load_x(v):
             nc.sync.dma_start(out=x_raw[v][:], in_=x_dram[v])
 
-        def load_scales(h):
+        def load_scales(v, h):
             for r in range(4):
                 nc.sync.dma_start(
-                    out=w_planes[h][r:PARTS:32, :, :].bitcast(I32),
-                    in_=s_dram[r][:, :, half(h)].bitcast(I32),
+                    out=w_planes[v][h][r:PARTS:32, :, :].bitcast(I32),
+                    in_=s_dram[v, r][:, :, half(h)].bitcast(I32),
                 )
 
         def load_words(v, h):
@@ -92,22 +95,25 @@ def tile_iwht3layer_pa_e_kernel(tc, trans, weight_words, weight_scales, bias, ou
 
         masks.make_identity(nc, ident[:])
         with tc.manual_schedule():
-            zero_planes(0)
+            zero_planes(0, 0)
             nc.vector.memset(bias_row[:], 0.0)
             nc.vector.memset(ones[:], 1.0)
-            zero_planes(1)
+            for h in range(HALVES):
+                for v in range(SIDE):
+                    if (v, h) != (0, 0):
+                        zero_planes(v, h)
             load_x(0)
             load_x(1)
-            load_scales(0)
+            load_scales(0, 0)
             nc.sync.dma_start(out=bias_row[0:1, :], in_=bias.rearrange("a b c k -> (a b c) k"))
             load_words(0, 0)
-            load_x(2)
-            load_words(1, 0)
-            load_x(3)
-            load_words(2, 0)
-            load_words(3, 0)
-            load_scales(1)
+            for v in range(1, SIDE):
+                load_scales(v, 0)
+                if v + 1 < SIDE:
+                    load_x(v + 1)
+                load_words(v, 0)
             for v in range(SIDE):
+                load_scales(v, 1)
                 load_words(v, 1)
 
         def quantise_x(v):
@@ -146,7 +152,7 @@ def tile_iwht3layer_pa_e_kernel(tc, trans, weight_words, weight_scales, bias, ou
                     lhsT=x_codes[v][:, sign, tokens].bitcast(FP8X4),
                     lhsT_scale=x_planes[v][:, sign, tokens],
                     rhs=w_words[v][h][:, u, :].bitcast(FP4X4),
-                    rhs_scale=w_planes[h][:, SIDE * u + v, :],
+                    rhs_scale=w_planes[v][h][:, u, :],
                     start=(u == 0),
                     stop=(u == SIDE - 1),
                 )

@@ -176,7 +176,7 @@ def tile_iwht3layer_pa_e_kernel(tc, trans, weight_words, weight_scales, bias, ou
 
         def step(p, v, h):
             number = SIDE * h + p
-            by_gpsimd = 0 if number == SIDE * HALVES - 1 else (4 if number % 2 == 0 else 2)
+            by_gpsimd = 4 if (number % 2 == 0 and number < SIDE * HALVES - 2) else 2
             chain = [q for q in range(SIDE) if by_gpsimd == 0 or (by_gpsimd == 2 and q % 2 == 1)]
             acc = mx_group(p, v, h)
             if v == 0:
@@ -225,6 +225,29 @@ def tile_iwht3layer_pa_e_kernel(tc, trans, weight_words, weight_scales, bias, ou
                 columns = slice(q * C_OUT + h * BANK, q * C_OUT + (h + 1) * BANK)
                 nc.sync.dma_start(out=out_dram[p][:, :, columns], in_=result[:, q, :])
 
+        def folded(p, h):
+            pair_low = low[(p, h)]
+            result = work.tile([PARTS, SIDE, BANK], F32, name="result")
+            for parity, sign_of_3 in ((0, 1), (1, -1)):
+                acc = psum.tile([PARTS, BANK], F32, name="acc", tag="bank")
+                for v, v_sign in ((2, 1), (3, sign_of_3)):
+                    for u in range(SIDE):
+                        sign = PLUS if HADAMARD[p][u] * v_sign > 0 else MINUS
+                        tokens = slice(u * PARTS, (u + 1) * PARTS)
+                        nc.tensor.matmul_mx(
+                            out=acc[:],
+                            lhsT=x_codes[v][:, sign, tokens].bitcast(FP8X4),
+                            lhsT_scale=x_planes[v][:, sign, tokens],
+                            rhs=w_words[v][h][:, u, :].bitcast(FP4X4),
+                            rhs_scale=w_planes[v][h][:, u, :],
+                            start=(v == 2 and u == 0),
+                            stop=(v == 3 and u == SIDE - 1),
+                        )
+                for q, factor in ((parity, 1.0 / 16.0), (parity + 2, -1.0 / 16.0)):
+                    scaled_sum(result[:, q, :], acc, factor, pair_low[:, parity, :])
+                    columns = slice(q * C_OUT + h * BANK, q * C_OUT + (h + 1) * BANK)
+                    nc.sync.dma_start(out=out_dram[p][:, :, columns], in_=result[:, q, :])
+
         FIRST = 2
         with tc.manual_schedule(engines={mybir.EngineType.PE}):
             quantise_x(0)
@@ -240,4 +263,6 @@ def tile_iwht3layer_pa_e_kernel(tc, trans, weight_words, weight_scales, bias, ou
                     step(p, v, 0)
             for p in range(SIDE):
                 for v in range(SIDE):
-                    step(p, v, 1)
+                    if p < SIDE - 1 or v < 2:
+                        step(p, v, 1)
+            folded(SIDE - 1, 1)

@@ -75,7 +75,10 @@ def tile_iwht3layer_pa_e_kernel(tc, trans, weight_words, weight_scales, bias, ou
         ]
 
         def zero_planes(v, h):
-            nc.vector.memset(w_planes[v][h][:].rearrange("p u n -> p (u n)").bitcast(I32), 0)
+            if (v, h) == (0, 0):
+                nc.vector.memset(w_planes[v][h][:].rearrange("p u n -> p (u n)").bitcast(I32), 0)
+            else:
+                nc.gpsimd.memset(w_planes[v][h][:].rearrange("p u n -> p (u n)").bitcast(F32), 0.0)
 
         def load_x(v):
             nc.sync.dma_start(out=x_raw[v][:], in_=x_dram[v])
@@ -95,17 +98,17 @@ def tile_iwht3layer_pa_e_kernel(tc, trans, weight_words, weight_scales, bias, ou
 
         masks.make_identity(nc, ident[:])
         with tc.manual_schedule():
-            zero_planes(0, 0)
             nc.vector.memset(bias_row[:], 0.0)
+            zero_planes(0, 0)
             nc.vector.memset(ones[:], 1.0)
             for h in range(HALVES):
                 for v in range(SIDE):
                     if (v, h) != (0, 0):
                         zero_planes(v, h)
             load_x(0)
+            nc.sync.dma_start(out=bias_row[0:1, :], in_=bias.rearrange("a b c k -> (a b c) k"))
             load_x(1)
             load_scales(0, 0)
-            nc.sync.dma_start(out=bias_row[0:1, :], in_=bias.rearrange("a b c k -> (a b c) k"))
             load_words(0, 0)
             for v in range(1, SIDE):
                 load_scales(v, 0)
@@ -133,14 +136,31 @@ def tile_iwht3layer_pa_e_kernel(tc, trans, weight_words, weight_scales, bias, ou
                 )
             x_plus_bf = x_plus[:].rearrange("p u t w -> p (u t w)").bitcast(BF16)
             x_minus = stage.tile([PARTS, SIDE * C_IN], BF16, name="x_minus", align_bytes=64)
-            for sign, values in ((PLUS, x_plus_bf), (MINUS, x_minus[:])):
-                if sign == MINUS:
-                    nc.vector.tensor_scalar_mul(out=x_minus[:], in0=x_plus_bf, scalar1=-1.0)
+
+            def quantise(sign, values, first, last):
+                words = slice(first * PARTS, last * PARTS)
                 nc.vector.quantize_mx(
-                    out=x_codes[v][:, sign, :].bitcast(FP8X4),
-                    scales=x_planes[v][:, sign, :],
-                    in_=values,
+                    out=x_codes[v][:, sign, words].bitcast(FP8X4),
+                    scales=x_planes[v][:, sign, words],
+                    in_=values[:, first * C_IN : last * C_IN],
                 )
+
+            quantise(PLUS, x_plus_bf, 0, SIDE)
+            first = 0 if v == SIDE - 1 else 1
+            columns = slice(first * C_IN, SIDE * C_IN)
+            if v != 1:
+                nc.vector.tensor_scalar_mul(
+                    out=x_minus[:, columns], in0=x_plus_bf[:, columns], scalar1=-1.0
+                )
+            else:
+                nc.scalar.activation(
+                    out=x_minus[:, columns], in_=x_plus_bf[:, columns], func=copy_fn, scale=-1.0
+                )
+            if first == 0:
+                quantise(MINUS, x_minus[:], 0, SIDE)
+            else:
+                quantise(MINUS, x_minus[:], 1, 3)
+                quantise(MINUS, x_minus[:], 3, 4)
 
         def mx_group(p, v, h):
             acc = psum.tile([PARTS, BANK], F32, name="acc", tag="bank")
@@ -163,6 +183,11 @@ def tile_iwht3layer_pa_e_kernel(tc, trans, weight_words, weight_scales, bias, ou
                 out=dst, in0=acc[:], scalar=factor, in1=other, op0=mult, op1=add
             )
 
+        def warm_up(count):
+            for i in range(count):
+                warm_bank = psum.tile([PARTS, PARTS], F32, name="warm_bank", tag="bank")
+                nc.tensor.matmul(out=warm_bank[:], lhsT=ident[:], rhs=ident[:], start=True, stop=True)
+
         def bias_everywhere():
             for h in range(HALVES):
                 bias_bank = psum.tile([PARTS, BANK], F32, name="bias_bank", tag="bank")
@@ -173,15 +198,56 @@ def tile_iwht3layer_pa_e_kernel(tc, trans, weight_words, weight_scales, bias, ou
 
         low = {}
         kept = {}
+        front = keep.tile([PARTS, 2, BANK], F32, name="front")
+        back = keep.tile([PARTS, 2, BANK], F32, name="back")
+        base = keep.tile([PARTS, SIDE, BANK], F32, name="base")
+
+        def pair_group(v, h, us, sign_of_last):
+            acc = psum.tile([PARTS, BANK], F32, name="acc", tag="bank")
+            for u, s in zip(us, (1, sign_of_last)):
+                sign = PLUS if s > 0 else MINUS
+                tokens = slice(u * PARTS, (u + 1) * PARTS)
+                nc.tensor.matmul_mx(
+                    out=acc[:],
+                    lhsT=x_codes[v][:, sign, tokens].bitcast(FP8X4),
+                    lhsT_scale=x_planes[v][:, sign, tokens],
+                    rhs=w_words[v][h][:, u, :].bitcast(FP4X4),
+                    rhs_scale=w_planes[v][h][:, u, :],
+                    start=(u == us[0]),
+                    stop=(u == us[-1]),
+                )
+            return acc
+
+        def base_of_half(h):
+            for i, s in enumerate((1, -1)):
+                acc = pair_group(0, h, (0, 1), s)
+                scaled_sum(front[:, i, :], acc, 1.0 / 16.0, bias_all[:, half(h)])
+                acc = pair_group(0, h, (2, 3), s)
+                nc.scalar.activation(out=back[:, i, :], in_=acc[:], func=copy_fn, scale=1.0 / 16.0)
+            for p in range(SIDE):
+                nc.gpsimd.tensor_tensor(
+                    out=base[:, p, :],
+                    in0=front[:, p % 2, :],
+                    in1=back[:, p % 2, :],
+                    op=add if p < 2 else subtract,
+                )
 
         def step(p, v, h):
             number = SIDE * h + p
             by_gpsimd = 4 if (number % 2 == 0 and number < SIDE * HALVES - 2) else 2
             chain = [q for q in range(SIDE) if by_gpsimd == 0 or (by_gpsimd == 2 and q % 2 == 1)]
+            if v == 0 and h == 0:
+                return
             acc = mx_group(p, v, h)
             if v == 0:
                 low[(p, h)] = lows.tile([PARTS, 2, BANK], F32, name="low")
                 scaled_sum(low[(p, h)][:, 0, :], acc, 1.0 / 16.0, bias_all[:, half(h)])
+                return
+            if v == 1 and h == 0:
+                pair_low = lows.tile([PARTS, 2, BANK], F32, name="low")
+                low[(p, h)] = pair_low
+                scaled_sum(pair_low[:, 1, :], acc, -1.0 / 16.0, base[:, p, :])
+                scaled_sum(pair_low[:, 0, :], acc, 1.0 / 16.0, base[:, p, :])
                 return
             pair_low = low[(p, h)]
             if v == 1:
@@ -250,10 +316,13 @@ def tile_iwht3layer_pa_e_kernel(tc, trans, weight_words, weight_scales, bias, ou
 
         FIRST = 2
         with tc.manual_schedule(engines={mybir.EngineType.PE}):
+            warm_up(3)
             quantise_x(0)
             quantise_x(1)
             bias_everywhere()
             for v in range(SIDE):
+                if v == 0:
+                    base_of_half(0)
                 for p in range(FIRST):
                     step(p, v, 0)
                 if v + 2 < SIDE:

@@ -98,9 +98,9 @@ def tile_iwht3layer_pa_e_kernel(tc, trans, weight_words, weight_scales, bias, ou
 
         masks.make_identity(nc, ident[:])
         with tc.manual_schedule():
+            nc.vector.memset(ones[:], 1.0)
             nc.vector.memset(bias_row[:], 0.0)
             zero_planes(0, 0)
-            nc.vector.memset(ones[:], 1.0)
             for h in range(HALVES):
                 for v in range(SIDE):
                     if (v, h) != (0, 0):
@@ -148,14 +148,9 @@ def tile_iwht3layer_pa_e_kernel(tc, trans, weight_words, weight_scales, bias, ou
             quantise(PLUS, x_plus_bf, 0, SIDE)
             first = 0 if v == SIDE - 1 else 1
             columns = slice(first * C_IN, SIDE * C_IN)
-            if v != 1:
-                nc.vector.tensor_scalar_mul(
-                    out=x_minus[:, columns], in0=x_plus_bf[:, columns], scalar1=-1.0
-                )
-            else:
-                nc.scalar.activation(
-                    out=x_minus[:, columns], in_=x_plus_bf[:, columns], func=copy_fn, scale=-1.0
-                )
+            nc.vector.tensor_scalar_mul(
+                out=x_minus[:, columns], in0=x_plus_bf[:, columns], scalar1=-1.0
+            )
             if first == 0:
                 quantise(MINUS, x_minus[:], 0, SIDE)
             else:
@@ -186,7 +181,7 @@ def tile_iwht3layer_pa_e_kernel(tc, trans, weight_words, weight_scales, bias, ou
         def warm_up(count):
             for i in range(count):
                 warm_bank = psum.tile([PARTS, PARTS], F32, name="warm_bank", tag="bank")
-                nc.tensor.matmul(out=warm_bank[:], lhsT=ident[:], rhs=ident[:], start=True, stop=True)
+                nc.tensor.matmul(out=warm_bank[:], lhsT=ones[:], rhs=ones[:], start=True, stop=True)
 
         def bias_everywhere():
             for h in range(HALVES):
@@ -199,8 +194,6 @@ def tile_iwht3layer_pa_e_kernel(tc, trans, weight_words, weight_scales, bias, ou
         low = {}
         kept = {}
         front = keep.tile([PARTS, 2, BANK], F32, name="front")
-        back = keep.tile([PARTS, 2, BANK], F32, name="back")
-        base = keep.tile([PARTS, SIDE, BANK], F32, name="base")
 
         def pair_group(v, h, us, sign_of_last):
             acc = psum.tile([PARTS, BANK], F32, name="acc", tag="bank")
@@ -222,15 +215,11 @@ def tile_iwht3layer_pa_e_kernel(tc, trans, weight_words, weight_scales, bias, ou
             for i, s in enumerate((1, -1)):
                 acc = pair_group(0, h, (0, 1), s)
                 scaled_sum(front[:, i, :], acc, 1.0 / 16.0, bias_all[:, half(h)])
-                acc = pair_group(0, h, (2, 3), s)
-                nc.scalar.activation(out=back[:, i, :], in_=acc[:], func=copy_fn, scale=1.0 / 16.0)
+            back = [pair_group(0, h, (2, 3), s) for s in (1, -1)]
             for p in range(SIDE):
-                nc.gpsimd.tensor_tensor(
-                    out=base[:, p, :],
-                    in0=front[:, p % 2, :],
-                    in1=back[:, p % 2, :],
-                    op=add if p < 2 else subtract,
-                )
+                low[(p, h)] = lows.tile([PARTS, 2, BANK], F32, name="low")
+                factor = 1.0 / 16.0 if p < 2 else -1.0 / 16.0
+                scaled_sum(low[(p, h)][:, 0, :], back[p % 2], factor, front[:, p % 2, :])
 
         def step(p, v, h):
             number = SIDE * h + p
@@ -242,12 +231,6 @@ def tile_iwht3layer_pa_e_kernel(tc, trans, weight_words, weight_scales, bias, ou
             if v == 0:
                 low[(p, h)] = lows.tile([PARTS, 2, BANK], F32, name="low")
                 scaled_sum(low[(p, h)][:, 0, :], acc, 1.0 / 16.0, bias_all[:, half(h)])
-                return
-            if v == 1 and h == 0:
-                pair_low = lows.tile([PARTS, 2, BANK], F32, name="low")
-                low[(p, h)] = pair_low
-                scaled_sum(pair_low[:, 1, :], acc, -1.0 / 16.0, base[:, p, :])
-                scaled_sum(pair_low[:, 0, :], acc, 1.0 / 16.0, base[:, p, :])
                 return
             pair_low = low[(p, h)]
             if v == 1:
@@ -316,7 +299,7 @@ def tile_iwht3layer_pa_e_kernel(tc, trans, weight_words, weight_scales, bias, ou
 
         FIRST = 2
         with tc.manual_schedule(engines={mybir.EngineType.PE}):
-            warm_up(3)
+            warm_up(24)
             quantise_x(0)
             quantise_x(1)
             bias_everywhere()

@@ -297,7 +297,7 @@ def tile_iwht3layer_pa_e_kernel(tc, trans, weight_words, weight_scales, bias, ou
                     columns = slice(q * C_OUT + h * BANK, q * C_OUT + (h + 1) * BANK)
                     nc.sync.dma_start(out=out_dram[p][:, :, columns], in_=result[:, q, :])
 
-        FIRST = 2
+        FIRST = (0, 2, 1, 1)
         with tc.manual_schedule(engines={mybir.EngineType.PE}):
             warm_up(24)
             quantise_x(0)
@@ -306,13 +306,14 @@ def tile_iwht3layer_pa_e_kernel(tc, trans, weight_words, weight_scales, bias, ou
             for v in range(SIDE):
                 if v == 0:
                     base_of_half(0)
-                for p in range(FIRST):
+                for p in range(FIRST[v]):
                     step(p, v, 0)
                 if v + 2 < SIDE:
                     quantise_x(v + 2)
-            for p in range(FIRST, SIDE):
-                for v in range(SIDE):
-                    step(p, v, 0)
+            for p in range(SIDE):
+                for v in range(1, SIDE):
+                    if p >= FIRST[v]:
+                        step(p, v, 0)
             for p in range(SIDE):
                 for v in range(SIDE):
                     if p < SIDE - 1 or v < 2:

@@ -40,6 +40,7 @@ def tile_iwht3layer_pa_e_kernel(tc, trans, weight_words, weight_scales, bias, ou
         keep = ctx.enter_context(tc.tile_pool(name="keep", bufs=1))
         stage = ctx.enter_context(tc.tile_pool(name="stage", bufs=2))
         work = ctx.enter_context(tc.tile_pool(name="work", bufs=3))
+        results = ctx.enter_context(tc.tile_pool(name="results", bufs=5))
         lows = ctx.enter_context(tc.tile_pool(name="lows", bufs=6))
         psum = ctx.enter_context(tc.psum_pool(name="psum", bufs=8))
 
@@ -148,9 +149,14 @@ def tile_iwht3layer_pa_e_kernel(tc, trans, weight_words, weight_scales, bias, ou
             quantise(PLUS, x_plus_bf, 0, SIDE)
             first = 0 if v == SIDE - 1 else 1
             columns = slice(first * C_IN, SIDE * C_IN)
-            nc.vector.tensor_scalar_mul(
-                out=x_minus[:, columns], in0=x_plus_bf[:, columns], scalar1=-1.0
-            )
+            if v in (0, 3):
+                nc.vector.tensor_scalar_mul(
+                    out=x_minus[:, columns], in0=x_plus_bf[:, columns], scalar1=-1.0
+                )
+            else:
+                nc.scalar.activation(
+                    out=x_minus[:, columns], in_=x_plus_bf[:, columns], func=copy_fn, scale=-1.0
+                )
             if first == 0:
                 quantise(MINUS, x_minus[:], 0, SIDE)
             else:
@@ -248,7 +254,7 @@ def tile_iwht3layer_pa_e_kernel(tc, trans, weight_words, weight_scales, bias, ou
                         scaled_sum(partial[:, q, :], acc, HADAMARD[q][2] / 16.0, pair_low[:, q % 2, :])
                     kept[(p, h, "partial")] = partial
                 return
-            result = work.tile([PARTS, SIDE, BANK], F32, name="result")
+            result = results.tile([PARTS, SIDE, BANK], F32, name="result")
             if by_gpsimd > 0:
                 third = kept[(p, h, "third")]
                 high = work.tile([PARTS, 2, BANK], F32, name="high")
@@ -276,7 +282,7 @@ def tile_iwht3layer_pa_e_kernel(tc, trans, weight_words, weight_scales, bias, ou
 
         def folded(p, h):
             pair_low = low[(p, h)]
-            result = work.tile([PARTS, SIDE, BANK], F32, name="result")
+            result = results.tile([PARTS, SIDE, BANK], F32, name="result")
             for parity, sign_of_3 in ((0, 1), (1, -1)):
                 acc = psum.tile([PARTS, BANK], F32, name="acc", tag="bank")
                 for v, v_sign in ((2, 1), (3, sign_of_3)):

@@ -229,7 +229,7 @@ def tile_iwht3layer_pa_e_kernel(tc, trans, weight_words, weight_scales, bias, ou
 
         def step(p, v, h):
             number = SIDE * h + p
-            by_gpsimd = 4 if (number % 2 == 0 and number < SIDE * HALVES - 2) else 2
+            by_gpsimd = 4 if p == 0 else 2
             chain = [q for q in range(SIDE) if by_gpsimd == 0 or (by_gpsimd == 2 and q % 2 == 1)]
             if v == 0 and h == 0:
                 return
@@ -303,7 +303,7 @@ def tile_iwht3layer_pa_e_kernel(tc, trans, weight_words, weight_scales, bias, ou
                     columns = slice(q * C_OUT + h * BANK, q * C_OUT + (h + 1) * BANK)
                     nc.sync.dma_start(out=out_dram[p][:, :, columns], in_=result[:, q, :])
 
-        FIRST = (0, 2, 1, 1)
+        FIRST = (0, 2, 2, 1)
         with tc.manual_schedule(engines={mybir.EngineType.PE}):
             warm_up(24)
             quantise_x(0)

@@ -146,17 +146,27 @@ def tile_iwht3layer_pa_e_kernel(tc, trans, weight_words, weight_scales, bias, ou
                     in_=values[:, first * C_IN : last * C_IN],
                 )
 
-            quantise(PLUS, x_plus_bf, 0, SIDE)
+            def negate(columns):
+                if v in (0, 3):
+                    nc.vector.tensor_scalar_mul(
+                        out=x_minus[:, columns], in0=x_plus_bf[:, columns], scalar1=-1.0
+                    )
+                else:
+                    nc.scalar.activation(
+                        out=x_minus[:, columns], in_=x_plus_bf[:, columns], func=copy_fn, scale=-1.0
+                    )
+
+            if v == 0:
+                quantise(PLUS, x_plus_bf, 0, 2)
+                negate(slice(C_IN, 2 * C_IN))
+                quantise(MINUS, x_minus[:], 1, 2)
+                quantise(PLUS, x_plus_bf, 2, 4)
+                negate(slice(2 * C_IN, 4 * C_IN))
+                quantise(MINUS, x_minus[:], 2, 4)
+                return
             first = 0 if v == SIDE - 1 else 1
-            columns = slice(first * C_IN, SIDE * C_IN)
-            if v in (0, 3):
-                nc.vector.tensor_scalar_mul(
-                    out=x_minus[:, columns], in0=x_plus_bf[:, columns], scalar1=-1.0
-                )
-            else:
-                nc.scalar.activation(
-                    out=x_minus[:, columns], in_=x_plus_bf[:, columns], func=copy_fn, scale=-1.0
-                )
+            quantise(PLUS, x_plus_bf, 0, SIDE)
+            negate(slice(first * C_IN, SIDE * C_IN))
             if first == 0:
                 quantise(MINUS, x_minus[:], 0, SIDE)
             else:
@@ -179,9 +189,9 @@ def tile_iwht3layer_pa_e_kernel(tc, trans, weight_words, weight_scales, bias, ou
                 )
             return acc
 
-        def scaled_sum(dst, acc, factor, other):
+        def scaled_sum(dst, acc, factor, other, op=add):
             nc.vector.scalar_tensor_tensor(
-                out=dst, in0=acc[:], scalar=factor, in1=other, op0=mult, op1=add
+                out=dst, in0=acc[:], scalar=factor, in1=other, op0=mult, op1=op
             )
 
         def warm_up(count):
@@ -217,6 +227,13 @@ def tile_iwht3layer_pa_e_kernel(tc, trans, weight_words, weight_scales, bias, ou
                 )
             return acc
 
+        def negative_beside(p, h):
+            if p > 0:
+                pair_low = low[(p, h)]
+                nc.scalar.activation(
+                    out=pair_low[:, 1, :], in_=pair_low[:, 0, :], func=copy_fn, scale=-1.0
+                )
+
         def base_of_half(h):
             for i, s in enumerate((1, -1)):
                 acc = pair_group(0, h, (0, 1), s)
@@ -226,19 +243,32 @@ def tile_iwht3layer_pa_e_kernel(tc, trans, weight_words, weight_scales, bias, ou
                 low[(p, h)] = lows.tile([PARTS, 2, BANK], F32, name="low")
                 factor = 1.0 / 16.0 if p < 2 else -1.0 / 16.0
                 scaled_sum(low[(p, h)][:, 0, :], back[p % 2], factor, front[:, p % 2, :])
+                negative_beside(p, h)
 
         def step(p, v, h):
+            if v > 0 or h > 0:
+                elementwise(p, v, h, mx_group(p, v, h))
+
+        def elementwise(p, v, h, acc):
             number = SIDE * h + p
             by_gpsimd = 4 if p == 0 else 2
             chain = [q for q in range(SIDE) if by_gpsimd == 0 or (by_gpsimd == 2 and q % 2 == 1)]
-            if v == 0 and h == 0:
-                return
-            acc = mx_group(p, v, h)
             if v == 0:
                 low[(p, h)] = lows.tile([PARTS, 2, BANK], F32, name="low")
                 scaled_sum(low[(p, h)][:, 0, :], acc, 1.0 / 16.0, bias_all[:, half(h)])
+                negative_beside(p, h)
                 return
             pair_low = low[(p, h)]
+            if v == 1 and p > 0:
+                nc.vector.scalar_tensor_tensor(
+                    out=pair_low[:],
+                    in0=acc[:].unsqueeze(1).to_broadcast([PARTS, 2, BANK]),
+                    scalar=1.0 / 16.0,
+                    in1=pair_low[:],
+                    op0=mult,
+                    op1=add,
+                )
+                return
             if v == 1:
                 scaled_sum(pair_low[:, 1, :], acc, -1.0 / 16.0, pair_low[:, 0, :])
                 scaled_sum(pair_low[:, 0, :], acc, 1.0 / 16.0, pair_low[:, 0, :])
@@ -251,7 +281,9 @@ def tile_iwht3layer_pa_e_kernel(tc, trans, weight_words, weight_scales, bias, ou
                 if chain:
                     partial = work.tile([PARTS, SIDE, BANK], F32, name="partial")
                     for q in chain:
-                        scaled_sum(partial[:, q, :], acc, HADAMARD[q][2] / 16.0, pair_low[:, q % 2, :])
+                        scaled_sum(
+                            partial[:, q, :], acc, HADAMARD[q][2] / 16.0, pair_low[:, 1, :], subtract
+                        )
                     kept[(p, h, "partial")] = partial
                 return
             result = results.tile([PARTS, SIDE, BANK], F32, name="result")
@@ -299,29 +331,38 @@ def tile_iwht3layer_pa_e_kernel(tc, trans, weight_words, weight_scales, bias, ou
                             stop=(v == 3 and u == SIDE - 1),
                         )
                 for q, factor in ((parity, 1.0 / 16.0), (parity + 2, -1.0 / 16.0)):
-                    scaled_sum(result[:, q, :], acc, factor, pair_low[:, parity, :])
+                    op = subtract if parity == 1 else add
+                    scaled_sum(result[:, q, :], acc, factor, pair_low[:, parity, :], op)
                     columns = slice(q * C_OUT + h * BANK, q * C_OUT + (h + 1) * BANK)
                     nc.sync.dma_start(out=out_dram[p][:, :, columns], in_=result[:, q, :])
 
         FIRST = (0, 2, 2, 1)
         with tc.manual_schedule(engines={mybir.EngineType.PE}):
-            warm_up(24)
+            warm_up(20)
             quantise_x(0)
             quantise_x(1)
             bias_everywhere()
             for v in range(SIDE):
                 if v == 0:
                     base_of_half(0)
+                if v == SIDE - 1:
+                    ahead = mx_group(2, 1, 0)
                 for p in range(FIRST[v]):
                     step(p, v, 0)
                 if v + 2 < SIDE:
                     quantise_x(v + 2)
             for p in range(SIDE):
                 for v in range(1, SIDE):
-                    if p >= FIRST[v]:
+                    if (p, v) == (2, 1):
+                        elementwise(p, v, 0, ahead)
+                    elif p >= FIRST[v]:
+                        if (p, v) == (SIDE - 1, SIDE - 1):
+                            step(0, 0, 1)
                         step(p, v, 0)
             for p in range(SIDE):
-                for v in range(SIDE):
+                for v in range(1, SIDE):
+                    if v == SIDE - 1 and p < SIDE - 1:
+                        step(p + 1, 0, 1)
                     if p < SIDE - 1 or v < 2:
                         step(p, v, 1)
             folded(SIDE - 1, 1)

from contextlib import ExitStack

import concourse.masks as masks
import concourse.mybir as mybir

F32 = mybir.dt.float32
BF16 = mybir.dt.bfloat16
I32 = mybir.dt.int32
U32 = mybir.dt.uint32
U8 = mybir.dt.uint8
FP8X4 = mybir.dt.float8_e4m3fn_x4
FP4X4 = mybir.dt.float4_e2m1fn_x4

PARTS = 128
SIDE = 4
C_IN = 512
C_OUT = 1024
BANK = 512
HALVES = C_OUT // BANK
WORDS = C_IN // 2
PLUS, MINUS = 0, 1
HADAMARD = ((1, 1, 1, 1), (1, -1, 1, -1), (1, 1, -1, -1), (1, -1, -1, 1))

FLOPS = 2 * SIDE * SIDE * PARTS * C_IN * C_OUT


def tile_iwht3layer_pa_e_kernel(tc, trans, weight_words, weight_scales, bias, out):
    nc = tc.nc
    mult = mybir.AluOpType.mult
    add = mybir.AluOpType.add
    subtract = mybir.AluOpType.subtract
    copy_fn = mybir.ActivationFunctionType.Copy

    x_dram = trans.rearrange("(u v) b i j c -> v (b i j) u c", v=SIDE)
    w_dram = weight_words.rearrange("(u v) p n -> v p u n", v=SIDE)
    s_dram = weight_scales.rearrange("(u v) (quad r) n -> v r quad u n", v=SIDE, r=4)
    out_dram = out.rearrange("b (i p) (j q) k -> p (b i) j (q k)", p=SIDE, q=SIDE)

    with ExitStack() as ctx:
        keep = ctx.enter_context(tc.tile_pool(name="keep", bufs=1))
        stage = ctx.enter_context(tc.tile_pool(name="stage", bufs=2))
        work = ctx.enter_context(tc.tile_pool(name="work", bufs=3))
        results = ctx.enter_context(tc.tile_pool(name="results", bufs=5))
        lows = ctx.enter_context(tc.tile_pool(name="lows", bufs=6))
        psum = ctx.enter_context(tc.psum_pool(name="psum", bufs=8))

        def half(h):
            return slice(h * BANK, (h + 1) * BANK)

        ident = keep.tile([PARTS, PARTS], F32, name="ident")
        ones = keep.tile([PARTS, PARTS], BF16, name="ones")
        bias_row = keep.tile([PARTS, C_OUT], BF16, name="bias_row")
        bias_all = keep.tile([PARTS, C_OUT], F32, name="bias_all")
        x_raw = [keep.tile([PARTS, SIDE, C_IN], BF16, name="x_raw%d" % v) for v in range(SIDE)]
        w_words = [
            [
                keep.tile([PARTS, SIDE, 2 * BANK], U8, name="w_words%d%d" % (v, h), align_bytes=64)
                for h in range(HALVES)
            ]
            for v in range(SIDE)
        ]
        w_planes = [
            [
                keep.tile([PARTS, SIDE, BANK], U8, name="w_planes%d%d" % (v, h), align_bytes=64)
                for h in range(HALVES)
            ]
            for v in range(SIDE)
        ]
        x_codes = [
            keep.tile([PARTS, 2, SIDE * PARTS], U32, name="x_codes%d" % v, align_bytes=64)
            for v in range(SIDE)
        ]
        x_planes = [
            keep.tile([PARTS, 2, SIDE * PARTS], U8, name="x_planes%d" % v, align_bytes=64)
            for v in range(SIDE)
        ]

        def zero_planes(v, h):
            if (v, h) == (0, 0):
                nc.vector.memset(w_planes[v][h][:].rearrange("p u n -> p (u n)").bitcast(I32), 0)
            else:
                nc.gpsimd.memset(w_planes[v][h][:].rearrange("p u n -> p (u n)").bitcast(F32), 0.0)

        def load_x(v):
            nc.sync.dma_start(out=x_raw[v][:], in_=x_dram[v])

        def load_scales(v, h):
            for r in range(4):
                nc.sync.dma_start(
                    out=w_planes[v][h][r:PARTS:32, :, :].bitcast(I32),
                    in_=s_dram[v, r][:, :, half(h)].bitcast(I32),
                )

        def load_words(v, h):
            nc.sync.dma_start(
                out=w_words[v][h][:].bitcast(I32),
                in_=w_dram[v][:, :, 2 * h * BANK : 2 * (h + 1) * BANK].bitcast(I32),
            )

        masks.make_identity(nc, ident[:])
        with tc.manual_schedule():
            nc.vector.memset(ones[:], 1.0)
            nc.vector.memset(bias_row[:], 0.0)
            zero_planes(0, 0)
            for h in range(HALVES):
                for v in range(SIDE):
                    if (v, h) != (0, 0):
                        zero_planes(v, h)
            load_x(0)
            nc.sync.dma_start(out=bias_row[0:1, :], in_=bias.rearrange("a b c k -> (a b c) k"))
            load_x(1)
            load_scales(0, 0)
            load_words(0, 0)
            for v in range(1, SIDE):
                load_scales(v, 0)
                if v + 1 < SIDE:
                    load_x(v + 1)
                load_words(v, 0)
            for v in range(SIDE):
                load_scales(v, 1)
                load_words(v, 1)

        def quantise_x(v):
            x_plus = stage.tile([PARTS, SIDE, PARTS, 2], F32, name="x_plus", align_bytes=64)
            for pair in range(SIDE // 2):
                x_bank = psum.tile([PARTS, 2, 2, PARTS], F32, name="x_bank", tag="bank")
                for s in range(2):
                    x_words = x_raw[v][:, 2 * pair + s, :].bitcast(F32)
                    for w in range(2):
                        nc.tensor.transpose(
                            out=x_bank[:, s, w, :], in_=x_words[:, w:WORDS:2], identity=ident[:]
                        )
                copy_out = nc.vector.tensor_copy if (pair == 0 and v == 0) else nc.scalar.copy
                copy_out(
                    out=x_plus[:, 2 * pair : 2 * pair + 2, :, :],
                    in_=x_bank[:].rearrange("p s w t -> p s t w"),
                )
            x_plus_bf = x_plus[:].rearrange("p u t w -> p (u t w)").bitcast(BF16)
            x_minus = stage.tile([PARTS, SIDE * C_IN], BF16, name="x_minus", align_bytes=64)

            def quantise(sign, values, first, last):
                words = slice(first * PARTS, last * PARTS)
                nc.vector.quantize_mx(
                    out=x_codes[v][:, sign, words].bitcast(FP8X4),
                    scales=x_planes[v][:, sign, words],
                    in_=values[:, first * C_IN : last * C_IN],
                )

            def negate(columns):
                if v in (0, 3):
                    nc.vector.tensor_scalar_mul(
                        out=x_minus[:, columns], in0=x_plus_bf[:, columns], scalar1=-1.0
                    )
                else:
                    nc.scalar.activation(
                        out=x_minus[:, columns], in_=x_plus_bf[:, columns], func=copy_fn, scale=-1.0
                    )

            if v == 0:
                quantise(PLUS, x_plus_bf, 0, 2)
                negate(slice(C_IN, 2 * C_IN))
                quantise(MINUS, x_minus[:], 1, 2)
                quantise(PLUS, x_plus_bf, 2, 4)
                negate(slice(2 * C_IN, 4 * C_IN))
                quantise(MINUS, x_minus[:], 2, 4)
                return
            first = 0 if v == SIDE - 1 else 1
            quantise(PLUS, x_plus_bf, 0, SIDE)
            negate(slice(first * C_IN, SIDE * C_IN))
            if first == 0:
                quantise(MINUS, x_minus[:], 0, SIDE)
            else:
                quantise(MINUS, x_minus[:], 1, 3)
                quantise(MINUS, x_minus[:], 3, 4)

        def mx_group(p, v, h):
            acc = psum.tile([PARTS, BANK], F32, name="acc", tag="bank")
            for u in range(SIDE):
                sign = PLUS if HADAMARD[p][u] > 0 else MINUS
                tokens = slice(u * PARTS, (u + 1) * PARTS)
                nc.tensor.matmul_mx(
                    out=acc[:],
                    lhsT=x_codes[v][:, sign, tokens].bitcast(FP8X4),
                    lhsT_scale=x_planes[v][:, sign, tokens],
                    rhs=w_words[v][h][:, u, :].bitcast(FP4X4),
                    rhs_scale=w_planes[v][h][:, u, :],
                    start=(u == 0),
                    stop=(u == SIDE - 1),
                )
            return acc

        def scaled_sum(dst, acc, factor, other, op=add):
            nc.vector.scalar_tensor_tensor(
                out=dst, in0=acc[:], scalar=factor, in1=other, op0=mult, op1=op
            )

        def warm_up(count):
            for i in range(count):
                warm_bank = psum.tile([PARTS, PARTS], F32, name="warm_bank", tag="bank")
                nc.tensor.matmul(out=warm_bank[:], lhsT=ones[:], rhs=ones[:], start=True, stop=True)

        def bias_everywhere():
            for h in range(HALVES):
                bias_bank = psum.tile([PARTS, BANK], F32, name="bias_bank", tag="bank")
                nc.tensor.matmul(
                    out=bias_bank[:], lhsT=ones[:], rhs=bias_row[:, half(h)], start=True, stop=True
                )
                nc.scalar.copy(out=bias_all[:, half(h)], in_=bias_bank[:])

        low = {}
        kept = {}
        front = keep.tile([PARTS, 2, BANK], F32, name="front")

        def pair_group(v, h, us, sign_of_last):
            acc = psum.tile([PARTS, BANK], F32, name="acc", tag="bank")
            for u, s in zip(us, (1, sign_of_last)):
                sign = PLUS if s > 0 else MINUS
                tokens = slice(u * PARTS, (u + 1) * PARTS)
                nc.tensor.matmul_mx(
                    out=acc[:],
                    lhsT=x_codes[v][:, sign, tokens].bitcast(FP8X4),
                    lhsT_scale=x_planes[v][:, sign, tokens],
                    rhs=w_words[v][h][:, u, :].bitcast(FP4X4),
                    rhs_scale=w_planes[v][h][:, u, :],
                    start=(u == us[0]),
                    stop=(u == us[-1]),
                )
            return acc

        def negative_beside(p, h):
            if p > 0:
                pair_low = low[(p, h)]
                nc.scalar.activation(
                    out=pair_low[:, 1, :], in_=pair_low[:, 0, :], func=copy_fn, scale=-1.0
                )

        def base_of_half(h):
            for i, s in enumerate((1, -1)):
                acc = pair_group(0, h, (0, 1), s)
                scaled_sum(front[:, i, :], acc, 1.0 / 16.0, bias_all[:, half(h)])
            back = [pair_group(0, h, (2, 3), s) for s in (1, -1)]
            for p in range(SIDE):
                low[(p, h)] = lows.tile([PARTS, 2, BANK], F32, name="low")
                factor = 1.0 / 16.0 if p < 2 else -1.0 / 16.0
                scaled_sum(low[(p, h)][:, 0, :], back[p % 2], factor, front[:, p % 2, :])
                negative_beside(p, h)

        def step(p, v, h):
            if v > 0 or h > 0:
                elementwise(p, v, h, mx_group(p, v, h))

        def elementwise(p, v, h, acc):
            number = SIDE * h + p
            by_gpsimd = 4 if p == 0 else 2
            chain = [q for q in range(SIDE) if by_gpsimd == 0 or (by_gpsimd == 2 and q % 2 == 1)]
            if v == 0:
                low[(p, h)] = lows.tile([PARTS, 2, BANK], F32, name="low")
                scaled_sum(low[(p, h)][:, 0, :], acc, 1.0 / 16.0, bias_all[:, half(h)])
                negative_beside(p, h)
                return
            pair_low = low[(p, h)]
            if v == 1 and p > 0:
                nc.vector.scalar_tensor_tensor(
                    out=pair_low[:],
                    in0=acc[:].unsqueeze(1).to_broadcast([PARTS, 2, BANK]),
                    scalar=1.0 / 16.0,
                    in1=pair_low[:],
                    op0=mult,
                    op1=add,
                )
                return
            if v == 1:
                scaled_sum(pair_low[:, 1, :], acc, -1.0 / 16.0, pair_low[:, 0, :])
                scaled_sum(pair_low[:, 0, :], acc, 1.0 / 16.0, pair_low[:, 0, :])
                return
            if v == 2:
                if by_gpsimd > 0:
                    third = work.tile([PARTS, BANK], F32, name="third")
                    nc.scalar.activation(out=third[:], in_=acc[:], func=copy_fn, scale=1.0 / 16.0)
                    kept[(p, h, "third")] = third
                if chain:
                    partial = work.tile([PARTS, SIDE, BANK], F32, name="partial")
                    for q in chain:
                        scaled_sum(
                            partial[:, q, :], acc, HADAMARD[q][2] / 16.0, pair_low[:, 1, :], subtract
                        )
                    kept[(p, h, "partial")] = partial
                return
            result = results.tile([PARTS, SIDE, BANK], F32, name="result")
            if by_gpsimd > 0:
                third = kept[(p, h, "third")]
                high = work.tile([PARTS, 2, BANK], F32, name="high")
                scaled_sum(high[:, 0, :], acc, 1.0 / 16.0, third[:])
                if by_gpsimd == 4:
                    scaled_sum(high[:, 1, :], acc, -1.0 / 16.0, third[:])
                    nc.gpsimd.tensor_tensor(
                        out=result[:, 0:2, :], in0=pair_low[:], in1=high[:], op=add
                    )
                    nc.gpsimd.tensor_tensor(
                        out=result[:, 2:4, :], in0=pair_low[:], in1=high[:], op=subtract
                    )
                else:
                    nc.gpsimd.tensor_tensor(
                        out=result[:, 0, :], in0=pair_low[:, 0, :], in1=high[:, 0, :], op=add
                    )
                    nc.gpsimd.tensor_tensor(
                        out=result[:, 2, :], in0=pair_low[:, 0, :], in1=high[:, 0, :], op=subtract
                    )
            for q in chain:
                scaled_sum(result[:, q, :], acc, HADAMARD[q][3] / 16.0, kept[(p, h, "partial")][:, q, :])
            for q in range(SIDE):
                columns = slice(q * C_OUT + h * BANK, q * C_OUT + (h + 1) * BANK)
                nc.sync.dma_start(out=out_dram[p][:, :, columns], in_=result[:, q, :])

        def folded(p, h):
            pair_low = low[(p, h)]
            result = results.tile([PARTS, SIDE, BANK], F32, name="result")
            for parity, sign_of_3 in ((0, 1), (1, -1)):
                acc = psum.tile([PARTS, BANK], F32, name="acc", tag="bank")
                for v, v_sign in ((2, 1), (3, sign_of_3)):
                    for u in range(SIDE):
                        sign = PLUS if HADAMARD[p][u] * v_sign > 0 else MINUS
                        tokens = slice(u * PARTS, (u + 1) * PARTS)
                        nc.tensor.matmul_mx(
                            out=acc[:],
                            lhsT=x_codes[v][:, sign, tokens].bitcast(FP8X4),
                            lhsT_scale=x_planes[v][:, sign, tokens],
                            rhs=w_words[v][h][:, u, :].bitcast(FP4X4),
                            rhs_scale=w_planes[v][h][:, u, :],
                            start=(v == 2 and u == 0),
                            stop=(v == 3 and u == SIDE - 1),
                        )
                for q, factor in ((parity, 1.0 / 16.0), (parity + 2, -1.0 / 16.0)):
                    op = subtract if parity == 1 else add
                    scaled_sum(result[:, q, :], acc, factor, pair_low[:, parity, :], op)
                    columns = slice(q * C_OUT + h * BANK, q * C_OUT + (h + 1) * BANK)
                    nc.sync.dma_start(out=out_dram[p][:, :, columns], in_=result[:, q, :])

        FIRST = (0, 2, 2, 1)
        with tc.manual_schedule(engines={mybir.EngineType.PE}):
            warm_up(20)
            quantise_x(0)
            quantise_x(1)
            bias_everywhere()
            for v in range(SIDE):
                if v == 0:
                    base_of_half(0)
                if v == SIDE - 1:
                    ahead = mx_group(2, 1, 0)
                for p in range(FIRST[v]):
                    step(p, v, 0)
                if v + 2 < SIDE:
                    quantise_x(v + 2)
            for p in range(SIDE):
                for v in range(1, SIDE):
                    if (p, v) == (2, 1):
                        elementwise(p, v, 0, ahead)
                    elif p >= FIRST[v]:
                        if (p, v) == (SIDE - 1, SIDE - 1):
                            step(0, 0, 1)
                        step(p, v, 0)
            for p in range(SIDE):
                for v in range(1, SIDE):
                    if v == SIDE - 1 and p < SIDE - 1:
                        step(p + 1, 0, 1)
                    if p < SIDE - 1 or v < 2:
                        step(p, v, 1)
            folded(SIDE - 1, 1)
